import numpy as np
import ml_dtypes


def mxq(x, axis, fmt="e4m3"):
    dtype, down = {"e4m3": (ml_dtypes.float8_e4m3fn, 7), "e5m2": (ml_dtypes.float8_e5m2, 14)}[fmt]
    v = np.moveaxis(np.asarray(x, np.float32).astype(ml_dtypes.bfloat16).astype(np.float64), axis, -1)
    blocks = v.reshape(v.shape[:-1] + (-1, 32))
    amax = np.abs(blocks).max(-1, keepdims=True)
    byte = np.maximum(np.where(amax > 0, np.frexp(amax)[1] - 1 + 127, 0) - down, 1)
    scale = np.exp2(byte - 127.0)
    codes = (blocks / scale).astype(np.float32).astype(dtype).astype(np.float64)
    return np.moveaxis((codes * scale).reshape(v.shape), -1, axis)


WIDE = False


def mx_kscale(k):
    if not WIDE:
        return np.ones(k)
    levels = np.array([20, -20, 10, -10, 0])
    a = np.random.permutation(np.resize(levels, k // 512 * 4)).reshape(k // 512, 4)
    idx = np.arange(k)
    return np.exp2(a[idx // 512, idx % 128 // 32])


BF16 = ml_dtypes.bfloat16


def bf(x):
    return np.asarray(x, np.float32).astype(BF16)


def f64(x):
    return np.asarray(x).astype(np.float64)


N, C, H, W, CO, KS, ST = 8, 64, 35, 35, 512, 4, 1
KK = KS * KS
F = C * KK
HO = (H - KS) // ST + 1
WO = (W - KS) // ST + 1
T = N * HO * WO


def col2im(d):
    d = d.reshape(C, KS, KS, N, HO, WO)
    gx = np.zeros((N, C, H, W))
    for i in range(KS):
        for j in range(KS):
            gx[:, :, i:i + ST * (HO - 1) + 1:ST, j:j + ST * (WO - 1) + 1:ST] += d[:, i, j].transpose(1, 0, 2, 3)
    return gx


def setup_inputs():
    u = mx_kscale(CO)
    x = np.random.standard_normal((N, C, H, W))
    weight = np.random.uniform(0.0, 1.0, (CO, F)) * 1.7 / np.sqrt(F) / u[:, None]
    bias = np.random.uniform(-1.0, 1.0, (CO, 1)) * 0.5
    g = np.random.standard_normal((N, CO, HO, WO)) * np.exp2(np.random.randint(-12, 1, (N, 1, HO, WO))) * 4.0 * u[None, :, None, None]
    return {"x": bf(x), "weight": bf(weight), "bias": bf(bias), "grad_out": bf(g)}


def reference(x, weight, bias, grad_out):
    gflat = f64(grad_out).transpose(1, 0, 2, 3).reshape(CO, T)
    d = mxq(f64(weight), 0, "e4m3").T @ mxq(gflat, 0, "e5m2")
    return col2im(d)

@@ -1,0 +1,198 @@
+from contextlib import ExitStack
+
+import concourse.mybir as mybir
+
+BF16 = mybir.dt.bfloat16
+F32 = mybir.dt.float32
+I32 = mybir.dt.int32
+U32 = mybir.dt.uint32
+U8 = mybir.dt.uint8
+E4X4 = mybir.dt.float8_e4m3fn_x4
+E5X4 = mybir.dt.float8_e5m2_x4
+ADD = mybir.AluOpType.add
+
+P = 128
+PACK = 4
+N_IMG = 8
+C = 64
+CO = 512
+HG = 32
+HX = 35
+KS = 4
+PAIRS = N_IMG // 2
+ROWW = 64
+PERIOD = 36
+LEAD = KS - 1
+WIN_ROWS = 8
+WIN = WIN_ROWS * ROWW
+N_WIN = PAIRS * PERIOD // WIN_ROWS
+PLANE_ROWS = PAIRS * PERIOD + LEAD
+PLANE = PLANE_ROWS * ROWW
+CHUNK_ROWS = 16
+IMG = HX * HX
+IMG_PITCH = 1232
+
+FLOPS = 2 * CO * C * KS * KS * N_IMG * HG * HG
+BYTES = CO * C * KS * KS * 2 + N_IMG * CO * HG * HG * 2 + N_IMG * C * IMG * 4
+
+
+def tile_sparseconv2d_t_kernel(tc, x, weight, bias, grad_out, out):
+    nc = tc.nc
+    with ExitStack() as ctx:
+        keep = ctx.enter_context(tc.tile_pool(name="keep", bufs=1))
+        rawp = ctx.enter_context(tc.tile_pool(name="rawp", bufs=4))
+        grpp = ctx.enter_context(tc.tile_pool(name="grpp", bufs=3))
+        mrgp = ctx.enter_context(tc.tile_pool(name="mrgp", bufs=2))
+        psum = ctx.enter_context(tc.psum_pool(name="psum", bufs=8))
+
+        g_codes = keep.tile([P, PLANE], U32, align_bytes=64)
+        g_scales = keep.tile([P, PLANE], U8, align_bytes=64)
+        w_raw = keep.tile([P, PACK, C * KS * KS], BF16)
+        w_grp = keep.tile([P, 2, KS, C, 2, PACK], BF16, align_bytes=64)
+        w_codes = keep.tile([P, 2 * KS * P], U32, align_bytes=64)
+        w_scales = keep.tile([P, 2 * KS * P], U8, align_bytes=64)
+        sums = keep.tile([P, N_IMG, IMG_PITCH], F32)
+
+        def img_base(pair):
+            return 4 * (pair % 2)
+
+        def sums_view(pair):
+            b = img_base(pair)
+            return sums[:, 2 * pair : 2 * pair + 2, b : b + IMG].rearrange(
+                "p n (h w) -> p n h w", w=HX
+            )
+
+        zero_spans = [(0, LEAD)]
+        for pair in range(PAIRS):
+            zero_spans.append((PERIOD * pair + LEAD + HG, PERIOD * (pair + 1) + LEAD))
+        for r0, r1 in zero_spans:
+            nc.vector.memset(g_codes[:, r0 * ROWW : r1 * ROWW].bitcast(I32), 0)
+            nc.vector.memset(g_scales[:, r0 * ROWW : r1 * ROWW].bitcast(I32), 0)
+        for pair in range(PAIRS):
+            nc.vector.memset(sums_view(pair)[:, :, :, HG - 1 : HX], 0.0)
+
+        raws = {}
+
+        def load_image(n, halves):
+            raw = rawp.tile([P, PACK, HG * HG], BF16, name="raw")
+            src = grad_out[n].rearrange("(p t) h w -> p t (h w)", t=PACK)
+            step = HG * HG // halves
+            for s in range(halves):
+                nc.sync.dma_start(
+                    out=raw[:, :, s * step : (s + 1) * step],
+                    in_=src[:, :, s * step : (s + 1) * step],
+                )
+            raws[n] = raw
+
+        load_image(0, 1)
+        load_image(1, 1)
+        nc.sync.dma_start(out=w_raw[:], in_=weight.rearrange("(p t) f -> p t f", t=PACK))
+        load_image(2, 1)
+        load_image(3, 1)
+
+        w_src = w_raw[:].rearrange("p t (c i a b) -> p t c i a b", i=KS, a=2, b=2)
+        for jp in range(2):
+            for i in range(KS):
+                src = w_src[:, :, :, i, jp, :].rearrange("p t c b -> p c b t")
+                if i % 2 == 0:
+                    nc.vector.tensor_copy(out=w_grp[:, jp, i], in_=src)
+                else:
+                    nc.scalar.copy(out=w_grp[:, jp, i], in_=src)
+            cols = slice(jp * KS * P, (jp + 1) * KS * P)
+            nc.vector.quantize_mx(
+                out=w_codes[:, cols].bitcast(E4X4),
+                scales=w_scales[:, cols],
+                in_=w_grp[:, jp].rearrange("p i c b t -> p (i c b t)"),
+            )
+
+        def prepare_chunk(chunk):
+            pair, hf = divmod(chunk, 2)
+            grp = grpp.tile([P, CHUNK_ROWS, 2, HG, PACK], BF16, name="grp", align_bytes=64)
+            for nl in range(2):
+                raw = raws[2 * pair + nl]
+                src = raw[:, :, hf * CHUNK_ROWS * HG : (hf + 1) * CHUNK_ROWS * HG].rearrange(
+                    "p t (r q) -> p r q t", q=HG
+                )
+                if nl == 0:
+                    nc.vector.tensor_copy(out=grp[:, :, nl], in_=src)
+                else:
+                    nc.scalar.copy(out=grp[:, :, nl], in_=src)
+            c0 = (PERIOD * pair + LEAD + CHUNK_ROWS * hf) * ROWW
+            cols = slice(c0, c0 + CHUNK_ROWS * ROWW)
+            nc.vector.quantize_mx(
+                out=g_codes[:, cols].bitcast(E5X4),
+                scales=g_scales[:, cols],
+                in_=grp[:].rearrange("p r n q t -> p (r n q t)"),
+            )
+            if hf == 1 and 2 * pair + 4 < N_IMG:
+                load_image(2 * pair + 4, 1)
+                load_image(2 * pair + 5, 1)
+
+        def chunk_of_row(row):
+            pair, off = divmod(row, PERIOD)
+            if pair >= PAIRS:
+                return 2 * PAIRS - 1
+            off = off - LEAD
+            if off < 0:
+                return 2 * pair - 1
+            return 2 * pair + min(off // CHUNK_ROWS, 1)
+
+        def window(k):
+            for jp in range(2):
+                acc = psum.tile([P, WIN], F32, name="acc")
+                for i in range(KS):
+                    c0 = WIN * k + ROWW * (LEAD - i)
+                    s0 = (jp * KS + i) * P
+                    nc.tensor.matmul_mx(
+                        out=acc[:],
+                        lhsT=w_codes[:, s0 : s0 + P].bitcast(E4X4),
+                        lhsT_scale=w_scales[:, s0 : s0 + P],
+                        rhs=g_codes[:, c0 : c0 + WIN].bitcast(E5X4),
+                        rhs_scale=g_scales[:, c0 : c0 + WIN],
+                        start=(i == 0),
+                        stop=(i == KS - 1),
+                    )
+                acc_v = acc[:].rearrange("p (r n q) -> p r n q", n=2, q=HG)
+                row = WIN_ROWS * k
+                while row < WIN_ROWS * (k + 1):
+                    pair, h0 = divmod(row, PERIOD)
+                    h1 = min(h0 + WIN_ROWS * (k + 1) - row, PERIOD)
+                    hv = min(h1, HX)
+                    if hv > h0:
+                        a = row - WIN_ROWS * k
+                        dst = sums_view(pair)[:, :, h0:hv, 2 * jp : 2 * jp + HG].rearrange(
+                            "p n h w -> p h n w"
+                        )
+                        srcp = acc_v[:, a : a + hv - h0]
+                        if jp == 0:
+                            nc.scalar.copy(out=dst, in_=srcp)
+                        else:
+                            nc.vector.tensor_tensor(out=dst, in0=srcp, in1=dst, op=ADD)
+                    row += h1 - h0
+
+        def finish_pair(pair):
+            b = img_base(pair)
+            even = mrgp.tile([P, IMG], F32, name="even")
+            odd = mrgp.tile([P, IMG], F32, name="odd")
+            for nl in range(2):
+                n = 2 * pair + nl
+                nc.sync.dma_start(out=even[nl:P:2, :], in_=sums[0:P:2, n, b : b + IMG])
+                nc.sync.dma_start(out=odd[nl:P:2, :], in_=sums[1:P:2, n, b : b + IMG])
+            nc.vector.tensor_tensor(
+                out=even[:, 1:IMG], in0=even[:, 1:IMG], in1=odd[:, 0 : IMG - 1], op=ADD
+            )
+            for nl in range(2):
+                n = 2 * pair + nl
+                nc.sync.dma_start(
+                    out=out[n].rearrange("c h w -> c (h w)"), in_=even[nl:P:2, :]
+                )
+
+        done_chunks = 0
+        for k in range(N_WIN):
+            need = chunk_of_row(WIN_ROWS * k + WIN_ROWS - 1 + LEAD)
+            while done_chunks <= need:
+                prepare_chunk(done_chunks)
+                done_chunks += 1
+            window(k)
+            if (WIN_ROWS * (k + 1)) // PERIOD > (WIN_ROWS * k) // PERIOD:
+                finish_pair((WIN_ROWS * k) // PERIOD)

@@ -28,7 +28,7 @@ WIN = WIN_ROWS * ROWW
 N_WIN = PAIRS * PERIOD // WIN_ROWS
 PLANE_ROWS = PAIRS * PERIOD + LEAD
 PLANE = PLANE_ROWS * ROWW
-CHUNK_ROWS = 16
+FIRST_ROWS = 8
 IMG = HX * HX
 IMG_PITCH = 1232
 
@@ -42,7 +42,7 @@ def tile_sparseconv2d_t_kernel(tc, x, weight, bias, grad_out, out):
         keep = ctx.enter_context(tc.tile_pool(name="keep", bufs=1))
         rawp = ctx.enter_context(tc.tile_pool(name="rawp", bufs=4))
         grpp = ctx.enter_context(tc.tile_pool(name="grpp", bufs=3))
-        mrgp = ctx.enter_context(tc.tile_pool(name="mrgp", bufs=2))
+        mrgp = ctx.enter_context(tc.tile_pool(name="mrgp", bufs=3))
         psum = ctx.enter_context(tc.psum_pool(name="psum", bufs=8))
 
         g_codes = keep.tile([P, PLANE], U32, align_bytes=64)
@@ -73,28 +73,28 @@ def tile_sparseconv2d_t_kernel(tc, x, weight, bias, grad_out, out):
 
         raws = {}
 
-        def load_image(n, halves):
-            raw = rawp.tile([P, PACK, HG * HG], BF16, name="raw")
+        def load_rows(n, r0, r1):
+            if r0 == 0:
+                raws[n] = rawp.tile([P, PACK, HG * HG], BF16, name="raw")
             src = grad_out[n].rearrange("(p t) h w -> p t (h w)", t=PACK)
-            step = HG * HG // halves
-            for s in range(halves):
-                nc.sync.dma_start(
-                    out=raw[:, :, s * step : (s + 1) * step],
-                    in_=src[:, :, s * step : (s + 1) * step],
-                )
-            raws[n] = raw
+            nc.sync.dma_start(
+                out=raws[n][:, :, r0 * HG : r1 * HG], in_=src[:, :, r0 * HG : r1 * HG]
+            )
 
-        load_image(0, 1)
-        load_image(1, 1)
+        load_rows(0, 0, FIRST_ROWS)
+        load_rows(1, 0, FIRST_ROWS)
         nc.sync.dma_start(out=w_raw[:], in_=weight.rearrange("(p t) f -> p t f", t=PACK))
-        load_image(2, 1)
-        load_image(3, 1)
+        load_rows(0, FIRST_ROWS, HG)
+        load_rows(1, FIRST_ROWS, HG)
+        load_rows(2, 0, HG)
+        load_rows(3, 0, HG)
 
         w_src = w_raw[:].rearrange("p t (c i a b) -> p t c i a b", i=KS, a=2, b=2)
-        for jp in range(2):
+
+        def prepare_weights(jp):
             for i in range(KS):
                 src = w_src[:, :, :, i, jp, :].rearrange("p t c b -> p c b t")
-                if i % 2 == 0:
+                if i < KS - 1:
                     nc.vector.tensor_copy(out=w_grp[:, jp, i], in_=src)
                 else:
                     nc.scalar.copy(out=w_grp[:, jp, i], in_=src)
@@ -105,37 +105,40 @@ def tile_sparseconv2d_t_kernel(tc, x, weight, bias, grad_out, out):
                 in_=w_grp[:, jp].rearrange("p i c b t -> p (i c b t)"),
             )
 
-        def prepare_chunk(chunk):
-            pair, hf = divmod(chunk, 2)
-            grp = grpp.tile([P, CHUNK_ROWS, 2, HG, PACK], BF16, name="grp", align_bytes=64)
+        chunks = [(0, r0, FIRST_ROWS) for r0 in range(0, HG, FIRST_ROWS)]
+        for pair in range(1, PAIRS):
+            chunks.extend([(pair, 0, HG // 2), (pair, HG // 2, HG // 2)])
+
+        def prepare_chunk(pair, r0, rows):
+            grp = grpp.tile([P, rows, 2, HG, PACK], BF16, name="grp", align_bytes=64)
             for nl in range(2):
-                raw = raws[2 * pair + nl]
-                src = raw[:, :, hf * CHUNK_ROWS * HG : (hf + 1) * CHUNK_ROWS * HG].rearrange(
-                    "p t (r q) -> p r q t", q=HG
-                )
+                src = raws[2 * pair + nl][:, :, r0 * HG : (r0 + rows) * HG]
                 if nl == 0:
-                    nc.vector.tensor_copy(out=grp[:, :, nl], in_=src)
+                    nc.vector.tensor_copy(
+                        out=grp[:, :, nl].rearrange("p r (c i) t -> p r c t i", i=4),
+                        in_=src.rearrange("p t (r c i) -> p r c t i", c=HG // 4, i=4),
+                    )
                 else:
-                    nc.scalar.copy(out=grp[:, :, nl], in_=src)
-            c0 = (PERIOD * pair + LEAD + CHUNK_ROWS * hf) * ROWW
-            cols = slice(c0, c0 + CHUNK_ROWS * ROWW)
+                    nc.scalar.copy(
+                        out=grp[:, :, nl], in_=src.rearrange("p t (r q) -> p r q t", q=HG)
+                    )
+            c0 = (PERIOD * pair + LEAD + r0) * ROWW
+            cols = slice(c0, c0 + rows * ROWW)
             nc.vector.quantize_mx(
                 out=g_codes[:, cols].bitcast(E5X4),
                 scales=g_scales[:, cols],
                 in_=grp[:].rearrange("p r n q t -> p (r n q t)"),
             )
-            if hf == 1 and 2 * pair + 4 < N_IMG:
-                load_image(2 * pair + 4, 1)
-                load_image(2 * pair + 5, 1)
+            if r0 + rows == HG and 2 * pair + 4 < N_IMG:
+                load_rows(2 * pair + 4, 0, HG)
+                load_rows(2 * pair + 5, 0, HG)
 
-        def chunk_of_row(row):
-            pair, off = divmod(row, PERIOD)
-            if pair >= PAIRS:
-                return 2 * PAIRS - 1
-            off = off - LEAD
-            if off < 0:
-                return 2 * pair - 1
-            return 2 * pair + min(off // CHUNK_ROWS, 1)
+        def chunks_needed(row):
+            count = 0
+            for pair, r0, rows in chunks:
+                if PERIOD * pair + LEAD + r0 <= row:
+                    count += 1
+            return count
 
         def window(k):
             for jp in range(2):
@@ -170,29 +173,37 @@ def tile_sparseconv2d_t_kernel(tc, x, weight, bias, grad_out, out):
                             nc.vector.tensor_tensor(out=dst, in0=srcp, in1=dst, op=ADD)
                     row += h1 - h0
 
-        def finish_pair(pair):
-            b = img_base(pair)
-            even = mrgp.tile([P, IMG], F32, name="even")
-            odd = mrgp.tile([P, IMG], F32, name="odd")
+        def finish_rows(pair, h0, h1):
+            f0 = img_base(pair) + h0 * HX
+            size = (h1 - h0) * HX
+            even = mrgp.tile([P, size], F32, name="even")
+            odd = mrgp.tile([P, size], F32, name="odd")
             for nl in range(2):
                 n = 2 * pair + nl
-                nc.sync.dma_start(out=even[nl:P:2, :], in_=sums[0:P:2, n, b : b + IMG])
-                nc.sync.dma_start(out=odd[nl:P:2, :], in_=sums[1:P:2, n, b : b + IMG])
+                nc.sync.dma_start(out=even[nl:P:2, :], in_=sums[0:P:2, n, f0 : f0 + size])
+                nc.sync.dma_start(out=odd[nl:P:2, :], in_=sums[1:P:2, n, f0 : f0 + size])
             nc.vector.tensor_tensor(
-                out=even[:, 1:IMG], in0=even[:, 1:IMG], in1=odd[:, 0 : IMG - 1], op=ADD
+                out=even[:, 1:size], in0=even[:, 1:size], in1=odd[:, 0 : size - 1], op=ADD
             )
             for nl in range(2):
                 n = 2 * pair + nl
                 nc.sync.dma_start(
-                    out=out[n].rearrange("c h w -> c (h w)"), in_=even[nl:P:2, :]
+                    out=out[n].rearrange("c h w -> c (h w)")[:, h0 * HX : h1 * HX],
+                    in_=even[nl:P:2, :],
                 )
+
+        finish_after = {4: [(0, 0, HX)], 8: [(1, 0, HX)], 13: [(2, 0, HX)],
+                        15: [(3, 0, 20)], 16: [(3, 20, 28)], 17: [(3, 28, HX)]}
 
         done_chunks = 0
         for k in range(N_WIN):
-            need = chunk_of_row(WIN_ROWS * k + WIN_ROWS - 1 + LEAD)
-            while done_chunks <= need:
-                prepare_chunk(done_chunks)
+            need = chunks_needed(WIN_ROWS * k + WIN_ROWS - 1 + LEAD)
+            while done_chunks < need:
+                prepare_chunk(*chunks[done_chunks])
                 done_chunks += 1
+                if done_chunks == 1:
+                    prepare_weights(0)
+                    prepare_weights(1)
             window(k)
-            if (WIN_ROWS * (k + 1)) // PERIOD > (WIN_ROWS * k) // PERIOD:
-                finish_pair((WIN_ROWS * k) // PERIOD)
+            for part in finish_after.get(k, []):
+                finish_rows(*part)

@@ -29,11 +29,11 @@ N_WIN = PAIRS * PERIOD // WIN_ROWS
 PLANE_ROWS = PAIRS * PERIOD + LEAD
 PLANE = PLANE_ROWS * ROWW
 FIRST_ROWS = 8
-IMG = HX * HX
-IMG_PITCH = 1232
+SLOTS = 5
+SLOT = WIN_ROWS * HX
 
 FLOPS = 2 * CO * C * KS * KS * N_IMG * HG * HG
-BYTES = CO * C * KS * KS * 2 + N_IMG * CO * HG * HG * 2 + N_IMG * C * IMG * 4
+BYTES = CO * C * KS * KS * 2 + N_IMG * CO * HG * HG * 2 + N_IMG * C * HX * HX * 4
 
 
 def tile_sparseconv2d_t_kernel(tc, x, weight, bias, grad_out, out):
@@ -41,6 +41,7 @@ def tile_sparseconv2d_t_kernel(tc, x, weight, bias, grad_out, out):
     with ExitStack() as ctx:
         keep = ctx.enter_context(tc.tile_pool(name="keep", bufs=1))
         rawp = ctx.enter_context(tc.tile_pool(name="rawp", bufs=4))
+        topp = ctx.enter_context(tc.tile_pool(name="topp", bufs=2))
         grpp = ctx.enter_context(tc.tile_pool(name="grpp", bufs=3))
         mrgp = ctx.enter_context(tc.tile_pool(name="mrgp", bufs=3))
         psum = ctx.enter_context(tc.psum_pool(name="psum", bufs=8))
@@ -51,35 +52,24 @@ def tile_sparseconv2d_t_kernel(tc, x, weight, bias, grad_out, out):
         w_grp = keep.tile([P, 2, KS, C, 2, PACK], BF16, align_bytes=64)
         w_codes = keep.tile([P, 2 * KS * P], U32, align_bytes=64)
         w_scales = keep.tile([P, 2 * KS * P], U8, align_bytes=64)
-        sums = keep.tile([P, N_IMG, IMG_PITCH], F32)
+        sums = [
+            keep.tile([P, SLOTS, 2, SLOT], F32, name="sums%d" % pair) for pair in range(PAIRS)
+        ]
 
-        def img_base(pair):
-            return 4 * (pair % 2)
-
-        def sums_view(pair):
-            b = img_base(pair)
-            return sums[:, 2 * pair : 2 * pair + 2, b : b + IMG].rearrange(
-                "p n (h w) -> p n h w", w=HX
-            )
-
-        zero_spans = [(0, LEAD)]
-        for pair in range(PAIRS):
-            zero_spans.append((PERIOD * pair + LEAD + HG, PERIOD * (pair + 1) + LEAD))
-        for r0, r1 in zero_spans:
-            nc.vector.memset(g_codes[:, r0 * ROWW : r1 * ROWW].bitcast(I32), 0)
-            nc.vector.memset(g_scales[:, r0 * ROWW : r1 * ROWW].bitcast(I32), 0)
-        for pair in range(PAIRS):
-            nc.vector.memset(sums_view(pair)[:, :, :, HG - 1 : HX], 0.0)
-
-        raws = {}
+        pieces = {}
 
         def load_rows(n, r0, r1):
-            if r0 == 0:
-                raws[n] = rawp.tile([P, PACK, HG * HG], BF16, name="raw")
+            pool = topp if r1 - r0 == FIRST_ROWS else rawp
+            raw = pool.tile([P, PACK, (r1 - r0) * HG], BF16, name="raw")
             src = grad_out[n].rearrange("(p t) h w -> p t (h w)", t=PACK)
-            nc.sync.dma_start(
-                out=raws[n][:, :, r0 * HG : r1 * HG], in_=src[:, :, r0 * HG : r1 * HG]
-            )
+            nc.sync.dma_start(out=raw[:], in_=src[:, :, r0 * HG : r1 * HG])
+            pieces[n] = pieces.get(n, []) + [(r0, r1, raw)]
+
+        def loaded_rows(n, r0, rows):
+            for a, b, raw in pieces[n]:
+                if a <= r0 and r0 + rows <= b:
+                    return raw[:, :, (r0 - a) * HG : (r0 - a + rows) * HG]
+            raise ValueError("rows not in one piece")
 
         load_rows(0, 0, FIRST_ROWS)
         load_rows(1, 0, FIRST_ROWS)
@@ -89,39 +79,55 @@ def tile_sparseconv2d_t_kernel(tc, x, weight, bias, grad_out, out):
         load_rows(2, 0, HG)
         load_rows(3, 0, HG)
 
+        zero_spans = [(0, LEAD)]
+        for pair in range(PAIRS):
+            zero_spans.append((PERIOD * pair + LEAD + HG, PERIOD * (pair + 1) + LEAD))
+        for r0, r1 in zero_spans:
+            nc.vector.memset(g_codes[:, r0 * ROWW : r1 * ROWW].bitcast(I32), 0)
+            nc.vector.memset(g_scales[:, r0 * ROWW : r1 * ROWW].bitcast(I32), 0)
+        for pair in range(PAIRS):
+            rows = sums[pair][:].rearrange("p s n (r w) -> p (s n r) w", w=HX)
+            nc.vector.memset(rows[:, :, HG - 1 : HX], 0.0)
+            if pair % 2 == 0:
+                nc.vector.memset(sums[pair][:, SLOTS - 1, :, 3 * HX : SLOT], 0.0)
+            else:
+                nc.vector.memset(sums[pair][:, 0, :, 0 : 4 * HX], 0.0)
+                nc.vector.memset(sums[pair][:, SLOTS - 1, :, 7 * HX : SLOT], 0.0)
+
         w_src = w_raw[:].rearrange("p t (c i a b) -> p t c i a b", i=KS, a=2, b=2)
 
-        def prepare_weights(jp):
-            for i in range(KS):
+        def prepare_weights(jp, ih):
+            for i in (2 * ih, 2 * ih + 1):
                 src = w_src[:, :, :, i, jp, :].rearrange("p t c b -> p c b t")
-                if i < KS - 1:
+                if i % 2 == 0:
                     nc.vector.tensor_copy(out=w_grp[:, jp, i], in_=src)
                 else:
                     nc.scalar.copy(out=w_grp[:, jp, i], in_=src)
-            cols = slice(jp * KS * P, (jp + 1) * KS * P)
+            c0 = (jp * KS + 2 * ih) * P
             nc.vector.quantize_mx(
-                out=w_codes[:, cols].bitcast(E4X4),
-                scales=w_scales[:, cols],
-                in_=w_grp[:, jp].rearrange("p i c b t -> p (i c b t)"),
+                out=w_codes[:, c0 : c0 + 2 * P].bitcast(E4X4),
+                scales=w_scales[:, c0 : c0 + 2 * P],
+                in_=w_grp[:, jp, 2 * ih : 2 * ih + 2].rearrange("p i c b t -> p (i c b t)"),
             )
 
         chunks = [(0, r0, FIRST_ROWS) for r0 in range(0, HG, FIRST_ROWS)]
         for pair in range(1, PAIRS):
             chunks.extend([(pair, 0, HG // 2), (pair, HG // 2, HG // 2)])
 
-        def prepare_chunk(pair, r0, rows):
+        def prepare_chunk(pair, r0, rows, v_rows):
             grp = grpp.tile([P, rows, 2, HG, PACK], BF16, name="grp", align_bytes=64)
             for nl in range(2):
-                src = raws[2 * pair + nl][:, :, r0 * HG : (r0 + rows) * HG]
-                if nl == 0:
-                    nc.vector.tensor_copy(
-                        out=grp[:, :, nl].rearrange("p r (c i) t -> p r c t i", i=4),
-                        in_=src.rearrange("p t (r c i) -> p r c t i", c=HG // 4, i=4),
-                    )
-                else:
-                    nc.scalar.copy(
-                        out=grp[:, :, nl], in_=src.rearrange("p t (r q) -> p r q t", q=HG)
-                    )
+                src = loaded_rows(2 * pair + nl, r0, rows)
+                nc.vector.tensor_copy(
+                    out=grp[:, 0:v_rows, nl].rearrange("p r (c i) t -> p r c t i", i=4),
+                    in_=src[:, :, 0 : v_rows * HG].rearrange(
+                        "p t (r c i) -> p r c t i", c=HG // 4, i=4
+                    ),
+                )
+                nc.scalar.copy(
+                    out=grp[:, v_rows:rows, nl],
+                    in_=src[:, :, v_rows * HG : rows * HG].rearrange("p t (r q) -> p r q t", q=HG),
+                )
             c0 = (PERIOD * pair + LEAD + r0) * ROWW
             cols = slice(c0, c0 + rows * ROWW)
             nc.vector.quantize_mx(
@@ -139,6 +145,9 @@ def tile_sparseconv2d_t_kernel(tc, x, weight, bias, grad_out, out):
                 if PERIOD * pair + LEAD + r0 <= row:
                     count += 1
             return count
+
+        def first_window(pair):
+            return PERIOD * pair // WIN_ROWS
 
         def window(k):
             for jp in range(2):
@@ -163,9 +172,10 @@ def tile_sparseconv2d_t_kernel(tc, x, weight, bias, grad_out, out):
                     hv = min(h1, HX)
                     if hv > h0:
                         a = row - WIN_ROWS * k
-                        dst = sums_view(pair)[:, :, h0:hv, 2 * jp : 2 * jp + HG].rearrange(
-                            "p n h w -> p h n w"
+                        slot = sums[pair][:, k - first_window(pair)].rearrange(
+                            "p n (r w) -> p r n w", w=HX
                         )
+                        dst = slot[:, a : a + hv - h0, :, 2 * jp : 2 * jp + HG]
                         srcp = acc_v[:, a : a + hv - h0]
                         if jp == 0:
                             nc.scalar.copy(out=dst, in_=srcp)
@@ -173,37 +183,53 @@ def tile_sparseconv2d_t_kernel(tc, x, weight, bias, grad_out, out):
                             nc.vector.tensor_tensor(out=dst, in0=srcp, in1=dst, op=ADD)
                     row += h1 - h0
 
-        def finish_rows(pair, h0, h1):
-            f0 = img_base(pair) + h0 * HX
-            size = (h1 - h0) * HX
-            even = mrgp.tile([P, size], F32, name="even")
-            odd = mrgp.tile([P, size], F32, name="odd")
+        def finish_slots(pair, s0, s1):
+            shift = PERIOD * pair - WIN_ROWS * first_window(pair)
+            h0 = max(WIN_ROWS * s0 - shift, 0)
+            h1 = min(WIN_ROWS * s1 - shift, HX)
+            v0 = (h0 + shift - WIN_ROWS * s0) * HX
+            v1 = (h1 + shift - WIN_ROWS * s0) * HX
+            even = mrgp.tile([P, s1 - s0, SLOT], F32, name="even")
+            odd = mrgp.tile([P, s1 - s0, SLOT], F32, name="odd")
             for nl in range(2):
-                n = 2 * pair + nl
-                nc.sync.dma_start(out=even[nl:P:2, :], in_=sums[0:P:2, n, f0 : f0 + size])
-                nc.sync.dma_start(out=odd[nl:P:2, :], in_=sums[1:P:2, n, f0 : f0 + size])
+                half = slice(C * nl, C * (nl + 1))
+                nc.sync.dma_start(out=even[half], in_=sums[pair][0:P:2, s0:s1, nl, :])
+                nc.sync.dma_start(out=odd[half], in_=sums[pair][1:P:2, s0:s1, nl, :])
+            even_f = even[:].rearrange("p s f -> p (s f)")
+            odd_f = odd[:].rearrange("p s f -> p (s f)")
             nc.vector.tensor_tensor(
-                out=even[:, 1:size], in0=even[:, 1:size], in1=odd[:, 0 : size - 1], op=ADD
+                out=even_f[:, v0 + 1 : v1],
+                in0=even_f[:, v0 + 1 : v1],
+                in1=odd_f[:, v0 : v1 - 1],
+                op=ADD,
             )
-            for nl in range(2):
-                n = 2 * pair + nl
-                nc.sync.dma_start(
-                    out=out[n].rearrange("c h w -> c (h w)")[:, h0 * HX : h1 * HX],
-                    in_=even[nl:P:2, :],
-                )
+            nc.sync.dma_start(
+                out=out[2 * pair : 2 * pair + 2].rearrange("n c h w -> (n c) (h w)")[
+                    :, h0 * HX : h1 * HX
+                ],
+                in_=even_f[:, v0:v1],
+            )
 
-        finish_after = {4: [(0, 0, HX)], 8: [(1, 0, HX)], 13: [(2, 0, HX)],
-                        15: [(3, 0, 20)], 16: [(3, 20, 28)], 17: [(3, 28, HX)]}
+        finish_after = {4: [(0, 0, SLOTS)], 8: [(1, 0, SLOTS)], 13: [(2, 0, SLOTS)],
+                        15: [(3, 0, 3)], 16: [(3, 3, 4)], 17: [(3, 4, SLOTS)]}
 
         done_chunks = 0
         for k in range(N_WIN):
             need = chunks_needed(WIN_ROWS * k + WIN_ROWS - 1 + LEAD)
             while done_chunks < need:
-                prepare_chunk(*chunks[done_chunks])
+                pair, r0, rows = chunks[done_chunks]
+                if done_chunks < 2:
+                    v_rows = 5
+                elif rows == FIRST_ROWS:
+                    v_rows = 3
+                else:
+                    v_rows = 7
+                prepare_chunk(pair, r0, rows, v_rows)
                 done_chunks += 1
                 if done_chunks == 1:
-                    prepare_weights(0)
-                    prepare_weights(1)
+                    for jp in range(2):
+                        for ih in range(2):
+                            prepare_weights(jp, ih)
             window(k)
             for part in finish_after.get(k, []):
-                finish_rows(*part)
+                finish_slots(*part)

@@ -31,6 +31,9 @@ PLANE = PLANE_ROWS * ROWW
 FIRST_ROWS = 8
 SLOTS = 5
 SLOT = WIN_ROWS * HX
+LATE_PARTS = ((0, 3), (3, 4), (4, 5))
+LOOKAHEAD = 2
+V_ROWS = {8: 3, 16: 6}
 
 FLOPS = 2 * CO * C * KS * KS * N_IMG * HG * HG
 BYTES = CO * C * KS * KS * 2 + N_IMG * CO * HG * HG * 2 + N_IMG * C * HX * HX * 4
@@ -55,6 +58,11 @@ def tile_sparseconv2d_t_kernel(tc, x, weight, bias, grad_out, out):
         sums = [
             keep.tile([P, SLOTS, 2, SLOT], F32, name="sums%d" % pair) for pair in range(PAIRS)
         ]
+
+        partner = {
+            s0: keep.tile([P, s1 - s0, 2, SLOT], F32, name="partner%d" % s0)
+            for s0, s1 in LATE_PARTS
+        }
 
         pieces = {}
 
@@ -87,12 +95,15 @@ def tile_sparseconv2d_t_kernel(tc, x, weight, bias, grad_out, out):
             nc.vector.memset(g_scales[:, r0 * ROWW : r1 * ROWW].bitcast(I32), 0)
         for pair in range(PAIRS):
             rows = sums[pair][:].rearrange("p s n (r w) -> p (s n r) w", w=HX)
-            nc.vector.memset(rows[:, :, HG - 1 : HX], 0.0)
             if pair % 2 == 0:
-                nc.vector.memset(sums[pair][:, SLOTS - 1, :, 3 * HX : SLOT], 0.0)
+                nc.gpsimd.memset(sums[pair][:, SLOTS - 1, :, 3 * HX : SLOT], 0.0)
             else:
-                nc.vector.memset(sums[pair][:, 0, :, 0 : 4 * HX], 0.0)
-                nc.vector.memset(sums[pair][:, SLOTS - 1, :, 7 * HX : SLOT], 0.0)
+                nc.gpsimd.memset(sums[pair][:, 0, :, 0 : 4 * HX], 0.0)
+                nc.gpsimd.memset(sums[pair][:, SLOTS - 1, :, 7 * HX : SLOT], 0.0)
+            nc.gpsimd.memset(rows[:, :, HG - 1 : HX], 0.0)
+
+        for s0, s1 in LATE_PARTS:
+            nc.gpsimd.memset(partner[s0][:], 0.0)
 
         w_src = w_raw[:].rearrange("p t (c i a b) -> p t c i a b", i=KS, a=2, b=2)
 
@@ -192,9 +203,8 @@ def tile_sparseconv2d_t_kernel(tc, x, weight, bias, grad_out, out):
             even = mrgp.tile([P, s1 - s0, SLOT], F32, name="even")
             odd = mrgp.tile([P, s1 - s0, SLOT], F32, name="odd")
             for nl in range(2):
-                half = slice(C * nl, C * (nl + 1))
-                nc.sync.dma_start(out=even[half], in_=sums[pair][0:P:2, s0:s1, nl, :])
-                nc.sync.dma_start(out=odd[half], in_=sums[pair][1:P:2, s0:s1, nl, :])
+                nc.sync.dma_start(out=even[nl:P:2], in_=sums[pair][0:P:2, s0:s1, nl, :])
+                nc.sync.dma_start(out=odd[nl:P:2], in_=sums[pair][1:P:2, s0:s1, nl, :])
             even_f = even[:].rearrange("p s f -> p (s f)")
             odd_f = odd[:].rearrange("p s f -> p (s f)")
             nc.vector.tensor_tensor(
@@ -203,28 +213,42 @@ def tile_sparseconv2d_t_kernel(tc, x, weight, bias, grad_out, out):
                 in1=odd_f[:, v0 : v1 - 1],
                 op=ADD,
             )
-            nc.sync.dma_start(
-                out=out[2 * pair : 2 * pair + 2].rearrange("n c h w -> (n c) (h w)")[
-                    :, h0 * HX : h1 * HX
-                ],
-                in_=even_f[:, v0:v1],
+            for nl in range(2):
+                nc.gpsimd.dma_start(
+                    out=out[2 * pair + nl].rearrange("c h w -> c (h w)")[:, h0 * HX : h1 * HX],
+                    in_=even_f[nl:P:2, v0:v1],
+                )
+
+        def finish_late_part(pair, s0, s1):
+            shift = PERIOD * pair - WIN_ROWS * first_window(pair)
+            nc.sync.dma_start(out=partner[s0][0:P:2], in_=sums[pair][1:P:2, s0:s1])
+            nc.vector.tensor_tensor(
+                out=sums[pair][:, s0:s1, :, 1:SLOT],
+                in0=sums[pair][:, s0:s1, :, 1:SLOT],
+                in1=partner[s0][:, :, :, 0 : SLOT - 1],
+                op=ADD,
             )
+            for s in range(s0, s1):
+                h0 = max(WIN_ROWS * s - shift, 0)
+                h1 = min(WIN_ROWS * (s + 1) - shift, HX)
+                v0 = (h0 + shift - WIN_ROWS * s) * HX
+                nc.sync.dma_start(
+                    out=out[2 * pair : 2 * pair + 2].rearrange("n c h w -> c n (h w)")[
+                        :, :, h0 * HX : h1 * HX
+                    ],
+                    in_=sums[pair][0:P:2, s, :, v0 : v0 + (h1 - h0) * HX],
+                )
 
         finish_after = {4: [(0, 0, SLOTS)], 8: [(1, 0, SLOTS)], 13: [(2, 0, SLOTS)],
-                        15: [(3, 0, 3)], 16: [(3, 3, 4)], 17: [(3, 4, SLOTS)]}
+                        }
+        late_after = {15: LATE_PARTS[0], 16: LATE_PARTS[1], 17: LATE_PARTS[2]}
 
         done_chunks = 0
         for k in range(N_WIN):
-            need = chunks_needed(WIN_ROWS * k + WIN_ROWS - 1 + LEAD)
+            need = chunks_needed(WIN_ROWS * (k + LOOKAHEAD) + WIN_ROWS - 1 + LEAD)
             while done_chunks < need:
                 pair, r0, rows = chunks[done_chunks]
-                if done_chunks < 2:
-                    v_rows = 5
-                elif rows == FIRST_ROWS:
-                    v_rows = 3
-                else:
-                    v_rows = 7
-                prepare_chunk(pair, r0, rows, v_rows)
+                prepare_chunk(pair, r0, rows, 5 if done_chunks == 0 else V_ROWS[rows])
                 done_chunks += 1
                 if done_chunks == 1:
                     for jp in range(2):
@@ -233,3 +257,5 @@ def tile_sparseconv2d_t_kernel(tc, x, weight, bias, grad_out, out):
             window(k)
             for part in finish_after.get(k, []):
                 finish_slots(*part)
+            if k in late_after:
+                finish_late_part(PAIRS - 1, *late_after[k])

@@ -7,255 +7,245 @@ F32 = mybir.dt.float32
 I32 = mybir.dt.int32
 U32 = mybir.dt.uint32
 U8 = mybir.dt.uint8
-E4X4 = mybir.dt.float8_e4m3fn_x4
-E5X4 = mybir.dt.float8_e5m2_x4
+E4M3_X4 = mybir.dt.float8_e4m3fn_x4
+E5M2_X4 = mybir.dt.float8_e5m2_x4
 ADD = mybir.AluOpType.add
 
 P = 128
 PACK = 4
-N_IMG = 8
-C = 64
-CO = 512
-HG = 32
-HX = 35
+N_IMG, C, CO = 8, 64, 512
 KS = 4
+HG = 32
+HX = HG + KS - 1
 PAIRS = N_IMG // 2
-ROWW = 64
-PERIOD = 36
+ROW_COLS = 2 * HG
 LEAD = KS - 1
+PERIOD = LEAD + HG + 1
 WIN_ROWS = 8
-WIN = WIN_ROWS * ROWW
+WIN_COLS = WIN_ROWS * ROW_COLS
 N_WIN = PAIRS * PERIOD // WIN_ROWS
-PLANE_ROWS = PAIRS * PERIOD + LEAD
-PLANE = PLANE_ROWS * ROWW
-FIRST_ROWS = 8
-SLOTS = 5
+PLANE_COLS = (PAIRS * PERIOD + LEAD) * ROW_COLS
+CHUNK_ROWS = 8
+HALF_ROWS = 2 * CHUNK_ROWS
+CHUNKS_PER_PAIR = HG // CHUNK_ROWS
+N_CHUNKS = PAIRS * CHUNKS_PER_PAIR
+N_HALVES = N_CHUNKS // 2
+HALVES_AHEAD = 4
+PAIR_WINS = 5
 SLOT = WIN_ROWS * HX
-LATE_PARTS = ((0, 3), (3, 4), (4, 5))
-LOOKAHEAD = 2
-V_ROWS = {8: 3, 16: 6}
+V_ROWS_START, V_ROWS = 5, 3
+COPY_AHEAD, QUANT_AHEAD = 3, 2
+MERGE_LAG = 2
 
 FLOPS = 2 * CO * C * KS * KS * N_IMG * HG * HG
 BYTES = CO * C * KS * KS * 2 + N_IMG * CO * HG * HG * 2 + N_IMG * C * HX * HX * 4
+
+
+def out_rows(pair, k0, k1):
+    h0 = max(WIN_ROWS * k0 - PERIOD * pair, 0)
+    h1 = min(WIN_ROWS * k1 - PERIOD * pair, HX)
+    return h0, h1, (PERIOD * pair + h0 - WIN_ROWS * k0) * HX
 
 
 def tile_sparseconv2d_t_kernel(tc, x, weight, bias, grad_out, out):
     nc = tc.nc
     with ExitStack() as ctx:
         keep = ctx.enter_context(tc.tile_pool(name="keep", bufs=1))
-        rawp = ctx.enter_context(tc.tile_pool(name="rawp", bufs=4))
-        topp = ctx.enter_context(tc.tile_pool(name="topp", bufs=2))
-        grpp = ctx.enter_context(tc.tile_pool(name="grpp", bufs=3))
-        mrgp = ctx.enter_context(tc.tile_pool(name="mrgp", bufs=3))
-        psum = ctx.enter_context(tc.psum_pool(name="psum", bufs=8))
+        loaded = ctx.enter_context(tc.tile_pool(name="loaded", bufs=2 * HALVES_AHEAD))
+        grouped = ctx.enter_context(tc.tile_pool(name="grouped", bufs=4))
+        merged = ctx.enter_context(tc.tile_pool(name="merged", bufs=2))
+        banks = ctx.enter_context(tc.psum_pool(name="banks", bufs=8))
+        ctx.enter_context(tc.manual_schedule())
 
-        g_codes = keep.tile([P, PLANE], U32, align_bytes=64)
-        g_scales = keep.tile([P, PLANE], U8, align_bytes=64)
+        g_codes = keep.tile([P, PLANE_COLS], U32, align_bytes=64)
+        g_scales = keep.tile([P, PLANE_COLS], U8, align_bytes=64)
         w_raw = keep.tile([P, PACK, C * KS * KS], BF16)
         w_grp = keep.tile([P, 2, KS, C, 2, PACK], BF16, align_bytes=64)
         w_codes = keep.tile([P, 2 * KS * P], U32, align_bytes=64)
         w_scales = keep.tile([P, 2 * KS * P], U8, align_bytes=64)
-        sums = [
-            keep.tile([P, SLOTS, 2, SLOT], F32, name="sums%d" % pair) for pair in range(PAIRS)
+        sums = keep.tile([P, N_WIN, 2, SLOT], F32)
+        parts = []
+        for pair in range(PAIRS - 1):
+            k0 = PERIOD * pair // WIN_ROWS
+            parts.append((pair, k0, k0 + PAIR_WINS))
+        last_parts = [
+            (PAIRS - 1, N_WIN - PAIR_WINS, N_WIN - 2),
+            (PAIRS - 1, N_WIN - 2, N_WIN - 1),
+            (PAIRS - 1, N_WIN - 1, N_WIN),
         ]
-
+        parts.extend(last_parts)
         partner = {
-            s0: keep.tile([P, s1 - s0, 2, SLOT], F32, name="partner%d" % s0)
-            for s0, s1 in LATE_PARTS
+            part: keep.tile([P, part[2] - part[1], 2, SLOT], F32, name="partner%d" % part[1])
+            for part in last_parts
         }
 
-        pieces = {}
+        raw = {}
+        grp = {}
+        acc = {}
+        halves = {}
 
-        def load_rows(n, r0, r1):
-            pool = topp if r1 - r0 == FIRST_ROWS else rawp
-            raw = pool.tile([P, PACK, (r1 - r0) * HG], BF16, name="raw")
-            src = grad_out[n].rearrange("(p t) h w -> p t (h w)", t=PACK)
-            nc.sync.dma_start(out=raw[:], in_=src[:, :, r0 * HG : r1 * HG])
-            pieces[n] = pieces.get(n, []) + [(r0, r1, raw)]
+        def load_half(half):
+            pair, hf = divmod(half, 2)
+            for img in range(2):
+                raw[half, img] = loaded.tile([P, PACK, HALF_ROWS * HG], BF16, name="raw")
+                rows = grad_out[2 * pair + img, :, hf * HALF_ROWS : (hf + 1) * HALF_ROWS, :]
+                nc.sync.dma_start(
+                    out=raw[half, img][:], in_=rows.rearrange("(p t) h w -> p t (h w)", t=PACK)
+                )
 
-        def loaded_rows(n, r0, rows):
-            for a, b, raw in pieces[n]:
-                if a <= r0 and r0 + rows <= b:
-                    return raw[:, :, (r0 - a) * HG : (r0 - a + rows) * HG]
-            raise ValueError("rows not in one piece")
-
-        load_rows(0, 0, FIRST_ROWS)
-        load_rows(1, 0, FIRST_ROWS)
-        nc.sync.dma_start(out=w_raw[:], in_=weight.rearrange("(p t) f -> p t f", t=PACK))
-        load_rows(0, FIRST_ROWS, HG)
-        load_rows(1, FIRST_ROWS, HG)
-        load_rows(2, 0, HG)
-        load_rows(3, 0, HG)
-
-        zero_spans = [(0, LEAD)]
-        for pair in range(PAIRS):
-            zero_spans.append((PERIOD * pair + LEAD + HG, PERIOD * (pair + 1) + LEAD))
-        for r0, r1 in zero_spans:
-            nc.vector.memset(g_codes[:, r0 * ROWW : r1 * ROWW].bitcast(I32), 0)
-            nc.vector.memset(g_scales[:, r0 * ROWW : r1 * ROWW].bitcast(I32), 0)
-        for pair in range(PAIRS):
-            rows = sums[pair][:].rearrange("p s n (r w) -> p (s n r) w", w=HX)
-            if pair % 2 == 0:
-                nc.gpsimd.memset(sums[pair][:, SLOTS - 1, :, 3 * HX : SLOT], 0.0)
-            else:
-                nc.gpsimd.memset(sums[pair][:, 0, :, 0 : 4 * HX], 0.0)
-                nc.gpsimd.memset(sums[pair][:, SLOTS - 1, :, 7 * HX : SLOT], 0.0)
-            nc.gpsimd.memset(rows[:, :, HG - 1 : HX], 0.0)
-
-        for s0, s1 in LATE_PARTS:
-            nc.gpsimd.memset(partner[s0][:], 0.0)
-
-        w_src = w_raw[:].rearrange("p t (c i a b) -> p t c i a b", i=KS, a=2, b=2)
-
-        def prepare_weights(jp, ih):
-            for i in (2 * ih, 2 * ih + 1):
-                src = w_src[:, :, :, i, jp, :].rearrange("p t c b -> p c b t")
-                if i % 2 == 0:
-                    nc.vector.tensor_copy(out=w_grp[:, jp, i], in_=src)
-                else:
-                    nc.scalar.copy(out=w_grp[:, jp, i], in_=src)
-            c0 = (jp * KS + 2 * ih) * P
-            nc.vector.quantize_mx(
-                out=w_codes[:, c0 : c0 + 2 * P].bitcast(E4X4),
-                scales=w_scales[:, c0 : c0 + 2 * P],
-                in_=w_grp[:, jp, 2 * ih : 2 * ih + 2].rearrange("p i c b t -> p (i c b t)"),
-            )
-
-        chunks = [(0, r0, FIRST_ROWS) for r0 in range(0, HG, FIRST_ROWS)]
-        for pair in range(1, PAIRS):
-            chunks.extend([(pair, 0, HG // 2), (pair, HG // 2, HG // 2)])
-
-        def prepare_chunk(pair, r0, rows, v_rows):
-            grp = grpp.tile([P, rows, 2, HG, PACK], BF16, name="grp", align_bytes=64)
-            for nl in range(2):
-                src = loaded_rows(2 * pair + nl, r0, rows)
+        def copy_chunk(j, v_rows):
+            half, part = divmod(j, 2)
+            grp[j] = grouped.tile([P, CHUNK_ROWS, 2, HG, PACK], BF16, name="grp", align_bytes=64)
+            for img in range(2):
+                src = raw[half, img][:, :, part * CHUNK_ROWS * HG : (part + 1) * CHUNK_ROWS * HG]
                 nc.vector.tensor_copy(
-                    out=grp[:, 0:v_rows, nl].rearrange("p r (c i) t -> p r c t i", i=4),
+                    out=grp[j][:, 0:v_rows, img].rearrange("p r (c i) t -> p r c t i", i=4),
                     in_=src[:, :, 0 : v_rows * HG].rearrange(
                         "p t (r c i) -> p r c t i", c=HG // 4, i=4
                     ),
                 )
                 nc.scalar.copy(
-                    out=grp[:, v_rows:rows, nl],
-                    in_=src[:, :, v_rows * HG : rows * HG].rearrange("p t (r q) -> p r q t", q=HG),
+                    out=grp[j][:, v_rows:CHUNK_ROWS, img].rearrange(
+                        "p r (c i) t -> p r c t i", i=4
+                    ),
+                    in_=src[:, :, v_rows * HG : CHUNK_ROWS * HG].rearrange(
+                        "p t (r c i) -> p r c t i", c=HG // 4, i=4
+                    ),
                 )
-            c0 = (PERIOD * pair + LEAD + r0) * ROWW
-            cols = slice(c0, c0 + rows * ROWW)
+            if part == 1 and half + HALVES_AHEAD < N_HALVES:
+                load_half(half + HALVES_AHEAD)
+
+        def quantise_chunk(j):
+            pair, part = divmod(j, CHUNKS_PER_PAIR)
+            c0 = (PERIOD * pair + LEAD + CHUNK_ROWS * part) * ROW_COLS
+            cols = slice(c0, c0 + CHUNK_ROWS * ROW_COLS)
             nc.vector.quantize_mx(
-                out=g_codes[:, cols].bitcast(E5X4),
+                out=g_codes[:, cols].bitcast(E5M2_X4),
                 scales=g_scales[:, cols],
-                in_=grp[:].rearrange("p r n q t -> p (r n q t)"),
+                in_=grp[j][:].rearrange("p r n q t -> p (r n q t)"),
             )
-            if r0 + rows == HG and 2 * pair + 4 < N_IMG:
-                load_rows(2 * pair + 4, 0, HG)
-                load_rows(2 * pair + 5, 0, HG)
 
-        def chunks_needed(row):
-            count = 0
-            for pair, r0, rows in chunks:
-                if PERIOD * pair + LEAD + r0 <= row:
-                    count += 1
-            return count
+        def prepare_weights(a, i0):
+            w_src = w_raw[:].rearrange("p t (c i a b) -> p t c i a b", i=KS, a=2, b=2)
+            nc.vector.tensor_copy(
+                out=w_grp[:, a, i0], in_=w_src[:, :, :, i0, a, :].rearrange("p t c b -> p c b t")
+            )
+            nc.scalar.copy(
+                out=w_grp[:, a, i0 + 1],
+                in_=w_src[:, :, :, i0 + 1, a, :].rearrange("p t c b -> p c b t"),
+            )
+            c0 = (a * KS + i0) * P
+            nc.vector.quantize_mx(
+                out=w_codes[:, c0 : c0 + 2 * P].bitcast(E4M3_X4),
+                scales=w_scales[:, c0 : c0 + 2 * P],
+                in_=w_grp[:, a, i0 : i0 + 2].rearrange("p i c b t -> p (i c b t)"),
+            )
 
-        def first_window(pair):
-            return PERIOD * pair // WIN_ROWS
-
-        def window(k):
-            for jp in range(2):
-                acc = psum.tile([P, WIN], F32, name="acc")
+        def matmuls(k):
+            for a in range(2):
+                acc[k, a] = banks.tile([P, WIN_COLS], F32, name="acc")
                 for i in range(KS):
-                    c0 = WIN * k + ROWW * (LEAD - i)
-                    s0 = (jp * KS + i) * P
+                    c0 = WIN_COLS * k + ROW_COLS * (LEAD - i)
+                    s0 = (a * KS + i) * P
                     nc.tensor.matmul_mx(
-                        out=acc[:],
-                        lhsT=w_codes[:, s0 : s0 + P].bitcast(E4X4),
+                        out=acc[k, a][:],
+                        lhsT=w_codes[:, s0 : s0 + P].bitcast(E4M3_X4),
                         lhsT_scale=w_scales[:, s0 : s0 + P],
-                        rhs=g_codes[:, c0 : c0 + WIN].bitcast(E5X4),
-                        rhs_scale=g_scales[:, c0 : c0 + WIN],
+                        rhs=g_codes[:, c0 : c0 + WIN_COLS].bitcast(E5M2_X4),
+                        rhs_scale=g_scales[:, c0 : c0 + WIN_COLS],
                         start=(i == 0),
                         stop=(i == KS - 1),
                     )
-                acc_v = acc[:].rearrange("p (r n q) -> p r n q", n=2, q=HG)
-                row = WIN_ROWS * k
-                while row < WIN_ROWS * (k + 1):
-                    pair, h0 = divmod(row, PERIOD)
-                    h1 = min(h0 + WIN_ROWS * (k + 1) - row, PERIOD)
-                    hv = min(h1, HX)
-                    if hv > h0:
-                        a = row - WIN_ROWS * k
-                        slot = sums[pair][:, k - first_window(pair)].rearrange(
-                            "p n (r w) -> p r n w", w=HX
-                        )
-                        dst = slot[:, a : a + hv - h0, :, 2 * jp : 2 * jp + HG]
-                        srcp = acc_v[:, a : a + hv - h0]
-                        if jp == 0:
-                            nc.scalar.copy(out=dst, in_=srcp)
-                        else:
-                            nc.vector.tensor_tensor(out=dst, in0=srcp, in1=dst, op=ADD)
-                    row += h1 - h0
 
-        def finish_slots(pair, s0, s1):
-            shift = PERIOD * pair - WIN_ROWS * first_window(pair)
-            h0 = max(WIN_ROWS * s0 - shift, 0)
-            h1 = min(WIN_ROWS * s1 - shift, HX)
-            v0 = (h0 + shift - WIN_ROWS * s0) * HX
-            v1 = (h1 + shift - WIN_ROWS * s0) * HX
-            even = mrgp.tile([P, s1 - s0, SLOT], F32, name="even")
-            odd = mrgp.tile([P, s1 - s0, SLOT], F32, name="odd")
-            for nl in range(2):
-                nc.sync.dma_start(out=even[nl:P:2], in_=sums[pair][0:P:2, s0:s1, nl, :])
-                nc.sync.dma_start(out=odd[nl:P:2], in_=sums[pair][1:P:2, s0:s1, nl, :])
-            even_f = even[:].rearrange("p s f -> p (s f)")
-            odd_f = odd[:].rearrange("p s f -> p (s f)")
-            nc.vector.tensor_tensor(
-                out=even_f[:, v0 + 1 : v1],
-                in0=even_f[:, v0 + 1 : v1],
-                in1=odd_f[:, v0 : v1 - 1],
-                op=ADD,
-            )
-            for nl in range(2):
-                nc.gpsimd.dma_start(
-                    out=out[2 * pair + nl].rearrange("c h w -> c (h w)")[:, h0 * HX : h1 * HX],
-                    in_=even_f[nl:P:2, v0:v1],
+        def evacuate(k):
+            slot = sums[:, k].rearrange("p n (r w) -> p r n w", w=HX)
+            for a in range(2):
+                src = acc[k, a][:].rearrange("p (r n q) -> p r n q", n=2, q=HG)
+                dst = slot[:, :, :, 2 * a : 2 * a + HG]
+                if a == 0:
+                    nc.scalar.copy(out=dst, in_=src)
+                else:
+                    nc.vector.tensor_tensor(out=dst, in0=src, in1=dst, op=ADD)
+
+        def start_merge(part):
+            pair, k0, k1 = part
+            if part in partner:
+                for b in range(2):
+                    nc.sync.dma_start(out=partner[part][b:P:2], in_=sums[1 - b : P : 2, k0:k1])
+                return
+            halves[part] = [
+                merged.tile([P, k1 - k0, SLOT], F32, name="half%d" % b) for b in range(2)
+            ]
+            for img in range(2):
+                for b in range(2):
+                    nc.sync.dma_start(
+                        out=halves[part][b][img:P:2], in_=sums[b:P:2, k0:k1, img, :]
+                    )
+
+        def finish_merge(part):
+            pair, k0, k1 = part
+            if part in partner:
+                nc.vector.tensor_tensor(
+                    out=sums[:, k0:k1, :, 1:SLOT],
+                    in0=sums[:, k0:k1, :, 1:SLOT],
+                    in1=partner[part][:, :, :, 0 : SLOT - 1],
+                    op=ADD,
                 )
-
-        def finish_late_part(pair, s0, s1):
-            shift = PERIOD * pair - WIN_ROWS * first_window(pair)
-            nc.sync.dma_start(out=partner[s0][0:P:2], in_=sums[pair][1:P:2, s0:s1])
+                for k in range(k0, k1):
+                    h0, h1, v0 = out_rows(pair, k, k + 1)
+                    nc.sync.dma_start(
+                        out=out[2 * pair : 2 * pair + 2].rearrange("n c h w -> c n (h w)")[
+                            :, :, h0 * HX : h1 * HX
+                        ],
+                        in_=sums[0:P:2, k, :, v0 : v0 + (h1 - h0) * HX],
+                    )
+                return
+            h0, h1, v0 = out_rows(pair, k0, k1)
+            v1 = v0 + (h1 - h0) * HX
+            even, odd = [half[:].rearrange("p s f -> p (s f)") for half in halves[part]]
             nc.vector.tensor_tensor(
-                out=sums[pair][:, s0:s1, :, 1:SLOT],
-                in0=sums[pair][:, s0:s1, :, 1:SLOT],
-                in1=partner[s0][:, :, :, 0 : SLOT - 1],
-                op=ADD,
+                out=even[:, v0 + 1 : v1], in0=even[:, v0 + 1 : v1], in1=odd[:, v0 : v1 - 1], op=ADD
             )
-            for s in range(s0, s1):
-                h0 = max(WIN_ROWS * s - shift, 0)
-                h1 = min(WIN_ROWS * (s + 1) - shift, HX)
-                v0 = (h0 + shift - WIN_ROWS * s) * HX
+            for img in range(2):
                 nc.sync.dma_start(
-                    out=out[2 * pair : 2 * pair + 2].rearrange("n c h w -> c n (h w)")[
-                        :, :, h0 * HX : h1 * HX
-                    ],
-                    in_=sums[pair][0:P:2, s, :, v0 : v0 + (h1 - h0) * HX],
+                    out=out[2 * pair + img].rearrange("c h w -> c (h w)"), in_=even[img:P:2, v0:v1]
                 )
 
-        finish_after = {4: [(0, 0, SLOTS)], 8: [(1, 0, SLOTS)], 13: [(2, 0, SLOTS)],
-                        }
-        late_after = {15: LATE_PARTS[0], 16: LATE_PARTS[1], 17: LATE_PARTS[2]}
+        load_half(0)
+        nc.sync.dma_start(out=w_raw[:], in_=weight.rearrange("(p t) f -> p t f", t=PACK))
+        for half in range(1, HALVES_AHEAD):
+            load_half(half)
 
-        done_chunks = 0
-        for k in range(N_WIN):
-            need = chunks_needed(WIN_ROWS * (k + LOOKAHEAD) + WIN_ROWS - 1 + LEAD)
-            while done_chunks < need:
-                pair, r0, rows = chunks[done_chunks]
-                prepare_chunk(pair, r0, rows, 5 if done_chunks == 0 else V_ROWS[rows])
-                done_chunks += 1
-                if done_chunks == 1:
-                    for jp in range(2):
-                        for ih in range(2):
-                            prepare_weights(jp, ih)
-            window(k)
-            for part in finish_after.get(k, []):
-                finish_slots(*part)
-            if k in late_after:
-                finish_late_part(PAIRS - 1, *late_after[k])
+        for pair in range(PAIRS + 1):
+            c0 = max(PERIOD * pair - 1, 0) * ROW_COLS
+            c1 = (PERIOD * pair + LEAD) * ROW_COLS
+            nc.vector.memset(g_codes[:, c0:c1].bitcast(I32), 0)
+            nc.vector.memset(g_scales[:, c0:c1].bitcast(I32), 0)
+        nc.vector.memset(
+            sums[:].rearrange("p k n (r w) -> p (k n r) w", w=HX)[:, :, HG - 1 : HX], 0.0
+        )
+
+        for j in range(QUANT_AHEAD):
+            copy_chunk(j, V_ROWS_START)
+        for j in range(QUANT_AHEAD):
+            quantise_chunk(j)
+        for a in range(2):
+            for i0 in range(0, KS, 2):
+                prepare_weights(a, i0)
+        for j in range(QUANT_AHEAD, COPY_AHEAD):
+            copy_chunk(j, V_ROWS)
+
+        for k in range(N_WIN + MERGE_LAG):
+            if k + COPY_AHEAD < N_CHUNKS:
+                copy_chunk(k + COPY_AHEAD, V_ROWS)
+            if k + QUANT_AHEAD < N_CHUNKS:
+                quantise_chunk(k + QUANT_AHEAD)
+            if k < N_WIN:
+                matmuls(k)
+                evacuate(k)
+            for part in parts:
+                if part[2] - 1 == k:
+                    start_merge(part)
+            for part in parts:
+                if part[2] - 1 == k - MERGE_LAG:
+                    finish_merge(part)

@@ -29,8 +29,6 @@ CHUNK_ROWS = 8
 HALF_ROWS = 2 * CHUNK_ROWS
 CHUNKS_PER_PAIR = HG // CHUNK_ROWS
 N_CHUNKS = PAIRS * CHUNKS_PER_PAIR
-N_HALVES = N_CHUNKS // 2
-HALVES_AHEAD = 4
 PAIR_WINS = 5
 SLOT = WIN_ROWS * HX
 V_ROWS_START, V_ROWS = 5, 3
@@ -51,9 +49,8 @@ def tile_sparseconv2d_t_kernel(tc, x, weight, bias, grad_out, out):
     nc = tc.nc
     with ExitStack() as ctx:
         keep = ctx.enter_context(tc.tile_pool(name="keep", bufs=1))
-        loaded = ctx.enter_context(tc.tile_pool(name="loaded", bufs=2 * HALVES_AHEAD))
         grouped = ctx.enter_context(tc.tile_pool(name="grouped", bufs=4))
-        merged = ctx.enter_context(tc.tile_pool(name="merged", bufs=2))
+        merged = ctx.enter_context(tc.tile_pool(name="merged", bufs=1))
         banks = ctx.enter_context(tc.psum_pool(name="banks", bufs=8))
         ctx.enter_context(tc.manual_schedule())
 
@@ -84,20 +81,20 @@ def tile_sparseconv2d_t_kernel(tc, x, weight, bias, grad_out, out):
         acc = {}
         halves = {}
 
-        def load_half(half):
-            pair, hf = divmod(half, 2)
-            for img in range(2):
-                raw[half, img] = loaded.tile([P, PACK, HALF_ROWS * HG], BF16, name="raw")
-                rows = grad_out[2 * pair + img, :, hf * HALF_ROWS : (hf + 1) * HALF_ROWS, :]
-                nc.sync.dma_start(
-                    out=raw[half, img][:], in_=rows.rearrange("(p t) h w -> p t (h w)", t=PACK)
-                )
+        def load_rows(n, r0, r1):
+            tile = keep.tile([P, PACK, (r1 - r0) * HG], BF16, name="raw%d_%d" % (n, r0))
+            nc.sync.dma_start(
+                out=tile[:],
+                in_=grad_out[n, :, r0:r1, :].rearrange("(p t) h w -> p t (h w)", t=PACK),
+            )
+            for r in range(r0, r1, CHUNK_ROWS):
+                raw[n, r] = tile[:, :, (r - r0) * HG : (r - r0 + CHUNK_ROWS) * HG]
 
         def copy_chunk(j, v_rows):
-            half, part = divmod(j, 2)
+            pair, part = divmod(j, CHUNKS_PER_PAIR)
             grp[j] = grouped.tile([P, CHUNK_ROWS, 2, HG, PACK], BF16, name="grp", align_bytes=64)
             for img in range(2):
-                src = raw[half, img][:, :, part * CHUNK_ROWS * HG : (part + 1) * CHUNK_ROWS * HG]
+                src = raw[2 * pair + img, CHUNK_ROWS * part]
                 nc.vector.tensor_copy(
                     out=grp[j][:, 0:v_rows, img].rearrange("p r (c i) t -> p r c t i", i=4),
                     in_=src[:, :, 0 : v_rows * HG].rearrange(
@@ -112,8 +109,6 @@ def tile_sparseconv2d_t_kernel(tc, x, weight, bias, grad_out, out):
                         "p t (r c i) -> p r c t i", c=HG // 4, i=4
                     ),
                 )
-            if part == 1 and half + HALVES_AHEAD < N_HALVES:
-                load_half(half + HALVES_AHEAD)
 
         def quantise_chunk(j):
             pair, part = divmod(j, CHUNKS_PER_PAIR)
@@ -211,10 +206,13 @@ def tile_sparseconv2d_t_kernel(tc, x, weight, bias, grad_out, out):
                     out=out[2 * pair + img].rearrange("c h w -> c (h w)"), in_=even[img:P:2, v0:v1]
                 )
 
-        load_half(0)
+        for n in range(2):
+            load_rows(n, 0, HALF_ROWS)
         nc.sync.dma_start(out=w_raw[:], in_=weight.rearrange("(p t) f -> p t f", t=PACK))
-        for half in range(1, HALVES_AHEAD):
-            load_half(half)
+        for n in range(2):
+            load_rows(n, HALF_ROWS, HG)
+        for n in range(2, N_IMG):
+            load_rows(n, 0, HG)
 
         for pair in range(PAIRS + 1):
             c0 = max(PERIOD * pair - 1, 0) * ROW_COLS

@@ -33,6 +33,7 @@ PAIR_WINS = 5
 SLOT = WIN_ROWS * HX
 V_ROWS_START, V_ROWS = 5, 3
 COPY_AHEAD, QUANT_AHEAD = 3, 2
+WARM_UP = 8
 MERGE_LAG = 2
 
 FLOPS = 2 * CO * C * KS * KS * N_IMG * HG * HG
@@ -207,11 +208,17 @@ def tile_sparseconv2d_t_kernel(tc, x, weight, bias, grad_out, out):
                 )
 
         for n in range(2):
-            load_rows(n, 0, HALF_ROWS)
+            load_rows(n, 0, CHUNK_ROWS)
         nc.sync.dma_start(out=w_raw[:], in_=weight.rearrange("(p t) f -> p t f", t=PACK))
         for n in range(2):
+            load_rows(n, CHUNK_ROWS, HALF_ROWS)
+        for n in range(2):
             load_rows(n, HALF_ROWS, HG)
-        for n in range(2, N_IMG):
+        for n in range(2, 4):
+            load_rows(n, 0, HALF_ROWS)
+        for n in range(2, 4):
+            load_rows(n, HALF_ROWS, HG)
+        for n in range(4, N_IMG):
             load_rows(n, 0, HG)
 
         for pair in range(PAIRS + 1):
@@ -223,15 +230,20 @@ def tile_sparseconv2d_t_kernel(tc, x, weight, bias, grad_out, out):
             sums[:].rearrange("p k n (r w) -> p (k n r) w", w=HX)[:, :, HG - 1 : HX], 0.0
         )
 
-        for j in range(QUANT_AHEAD):
-            copy_chunk(j, V_ROWS_START)
-        for j in range(QUANT_AHEAD):
-            quantise_chunk(j)
+        copy_chunk(0, V_ROWS_START)
+        warm = banks.tile([P, WIN_COLS], F32, name="acc")
+        warm_src = raw[0, 0].rearrange("p t x -> p (t x)")
+        for w_i in range(WARM_UP):
+            nc.tensor.matmul(
+                out=warm[:], lhsT=warm_src[:, 0:P], rhs=warm_src[:, 0:WIN_COLS], start=True, stop=True
+            )
+        quantise_chunk(0)
         for a in range(2):
             for i0 in range(0, KS, 2):
                 prepare_weights(a, i0)
-        for j in range(QUANT_AHEAD, COPY_AHEAD):
-            copy_chunk(j, V_ROWS)
+        copy_chunk(1, V_ROWS_START)
+        quantise_chunk(1)
+        copy_chunk(2, V_ROWS)
 
         for k in range(N_WIN + MERGE_LAG):
             if k + COPY_AHEAD < N_CHUNKS:

@@ -10,6 +10,7 @@ U8 = mybir.dt.uint8
 E4M3_X4 = mybir.dt.float8_e4m3fn_x4
 E5M2_X4 = mybir.dt.float8_e5m2_x4
 ADD = mybir.AluOpType.add
+MULT = mybir.AluOpType.mult
 
 P = 128
 PACK = 4
@@ -31,7 +32,8 @@ CHUNKS_PER_PAIR = HG // CHUNK_ROWS
 N_CHUNKS = PAIRS * CHUNKS_PER_PAIR
 PAIR_WINS = 5
 SLOT = WIN_ROWS * HX
-V_ROWS_START, V_ROWS = 5, 3
+SHARES_START = (("vector", 0, 0, 8), ("scalar", 1, 0, 4), ("gpsimd", 1, 4, 8))
+SHARES = (("vector", 0, 0, 4), ("gpsimd", 0, 4, 8), ("scalar", 1, 0, 8))
 COPY_AHEAD, QUANT_AHEAD = 3, 2
 WARM_UP = 8
 MERGE_LAG = 2
@@ -91,25 +93,28 @@ def tile_sparseconv2d_t_kernel(tc, x, weight, bias, grad_out, out):
             for r in range(r0, r1, CHUNK_ROWS):
                 raw[n, r] = tile[:, :, (r - r0) * HG : (r - r0 + CHUNK_ROWS) * HG]
 
-        def copy_chunk(j, v_rows):
+        def copy_chunk(j, shares):
             pair, part = divmod(j, CHUNKS_PER_PAIR)
             grp[j] = grouped.tile([P, CHUNK_ROWS, 2, HG, PACK], BF16, name="grp", align_bytes=64)
-            for img in range(2):
-                src = raw[2 * pair + img, CHUNK_ROWS * part]
-                nc.vector.tensor_copy(
-                    out=grp[j][:, 0:v_rows, img].rearrange("p r (c i) t -> p r c t i", i=4),
-                    in_=src[:, :, 0 : v_rows * HG].rearrange(
-                        "p t (r c i) -> p r c t i", c=HG // 4, i=4
-                    ),
-                )
-                nc.scalar.copy(
-                    out=grp[j][:, v_rows:CHUNK_ROWS, img].rearrange(
-                        "p r (c i) t -> p r c t i", i=4
-                    ),
-                    in_=src[:, :, v_rows * HG : CHUNK_ROWS * HG].rearrange(
-                        "p t (r c i) -> p r c t i", c=HG // 4, i=4
-                    ),
-                )
+            for engine, img, r0, r1 in shares:
+                src = raw[2 * pair + img, CHUNK_ROWS * part][:, :, r0 * HG : r1 * HG]
+                dst = grp[j][:, r0:r1, img]
+                if engine == "gpsimd":
+                    nc.gpsimd.tensor_scalar(
+                        out=dst,
+                        in0=src.rearrange("p t (r q) -> p r q t", q=HG),
+                        scalar1=1.0,
+                        scalar2=0.0,
+                        op0=MULT,
+                        op1=ADD,
+                    )
+                    continue
+                dst4 = dst.rearrange("p r (c i) t -> p r c t i", i=4)
+                src4 = src.rearrange("p t (r c i) -> p r c t i", c=HG // 4, i=4)
+                if engine == "vector":
+                    nc.vector.tensor_copy(out=dst4, in_=src4)
+                else:
+                    nc.scalar.copy(out=dst4, in_=src4)
 
         def quantise_chunk(j):
             pair, part = divmod(j, CHUNKS_PER_PAIR)
@@ -230,7 +235,7 @@ def tile_sparseconv2d_t_kernel(tc, x, weight, bias, grad_out, out):
             sums[:].rearrange("p k n (r w) -> p (k n r) w", w=HX)[:, :, HG - 1 : HX], 0.0
         )
 
-        copy_chunk(0, V_ROWS_START)
+        copy_chunk(0, SHARES_START)
         warm = banks.tile([P, WIN_COLS], F32, name="acc")
         warm_src = raw[0, 0].rearrange("p t x -> p (t x)")
         for w_i in range(WARM_UP):
@@ -241,13 +246,13 @@ def tile_sparseconv2d_t_kernel(tc, x, weight, bias, grad_out, out):
         for a in range(2):
             for i0 in range(0, KS, 2):
                 prepare_weights(a, i0)
-        copy_chunk(1, V_ROWS_START)
+        copy_chunk(1, SHARES_START)
         quantise_chunk(1)
-        copy_chunk(2, V_ROWS)
+        copy_chunk(2, SHARES)
 
         for k in range(N_WIN + MERGE_LAG):
             if k + COPY_AHEAD < N_CHUNKS:
-                copy_chunk(k + COPY_AHEAD, V_ROWS)
+                copy_chunk(k + COPY_AHEAD, SHARES)
             if k + QUANT_AHEAD < N_CHUNKS:
                 quantise_chunk(k + QUANT_AHEAD)
             if k < N_WIN:

@@ -22,21 +22,24 @@ PAIRS = N_IMG // 2
 ROW_COLS = 2 * HG
 LEAD = KS - 1
 PERIOD = LEAD + HG + 1
+FRONT = 1
 WIN_ROWS = 8
 WIN_COLS = WIN_ROWS * ROW_COLS
 N_WIN = PAIRS * PERIOD // WIN_ROWS
-PLANE_COLS = (PAIRS * PERIOD + LEAD) * ROW_COLS
+PLANE_ROWS = FRONT + PAIRS * PERIOD + LEAD
+PLANE_COLS = PLANE_ROWS * ROW_COLS
 CHUNK_ROWS = 8
-HALF_ROWS = 2 * CHUNK_ROWS
 CHUNKS_PER_PAIR = HG // CHUNK_ROWS
 N_CHUNKS = PAIRS * CHUNKS_PER_PAIR
 PAIR_WINS = 5
-SLOT = WIN_ROWS * HX
+PITCH = 36
+SLOT = WIN_ROWS * PITCH
+PAD = 4
 SHARES_START = (("vector", 0, 0, 8), ("scalar", 1, 0, 4), ("gpsimd", 1, 4, 8))
 SHARES = (("vector", 0, 0, 4), ("gpsimd", 0, 4, 8), ("scalar", 1, 0, 8))
 COPY_AHEAD, QUANT_AHEAD = 3, 2
-WARM_UP = 8
 MERGE_LAG = 2
+WARM_UP = 8
 
 FLOPS = 2 * CO * C * KS * KS * N_IMG * HG * HG
 BYTES = CO * C * KS * KS * 2 + N_IMG * CO * HG * HG * 2 + N_IMG * C * HX * HX * 4
@@ -45,7 +48,7 @@ BYTES = CO * C * KS * KS * 2 + N_IMG * CO * HG * HG * 2 + N_IMG * C * HX * HX * 
 def out_rows(pair, k0, k1):
     h0 = max(WIN_ROWS * k0 - PERIOD * pair, 0)
     h1 = min(WIN_ROWS * k1 - PERIOD * pair, HX)
-    return h0, h1, (PERIOD * pair + h0 - WIN_ROWS * k0) * HX
+    return h0, h1, PERIOD * pair + h0 - WIN_ROWS * k0
 
 
 def tile_sparseconv2d_t_kernel(tc, x, weight, bias, grad_out, out):
@@ -53,7 +56,7 @@ def tile_sparseconv2d_t_kernel(tc, x, weight, bias, grad_out, out):
     with ExitStack() as ctx:
         keep = ctx.enter_context(tc.tile_pool(name="keep", bufs=1))
         grouped = ctx.enter_context(tc.tile_pool(name="grouped", bufs=4))
-        merged = ctx.enter_context(tc.tile_pool(name="merged", bufs=1))
+        results = ctx.enter_context(tc.tile_pool(name="results", bufs=3))
         banks = ctx.enter_context(tc.psum_pool(name="banks", bufs=8))
         ctx.enter_context(tc.manual_schedule())
 
@@ -63,7 +66,10 @@ def tile_sparseconv2d_t_kernel(tc, x, weight, bias, grad_out, out):
         w_grp = keep.tile([P, 2, KS, C, 2, PACK], BF16, align_bytes=64)
         w_codes = keep.tile([P, 2 * KS * P], U32, align_bytes=64)
         w_scales = keep.tile([P, 2 * KS * P], U8, align_bytes=64)
-        sums = keep.tile([P, N_WIN, 2, SLOT], F32)
+        sums = keep.tile([P, N_WIN, 2, SLOT], F32, align_bytes=64)
+        half_even = keep.tile([P, PAIR_WINS * SLOT], F32, align_bytes=64)
+        half_odd = keep.tile([P, PAD + PAIR_WINS * SLOT], F32, align_bytes=64)
+
         parts = []
         for pair in range(PAIRS - 1):
             k0 = PERIOD * pair // WIN_ROWS
@@ -75,14 +81,15 @@ def tile_sparseconv2d_t_kernel(tc, x, weight, bias, grad_out, out):
         ]
         parts.extend(last_parts)
         partner = {
-            part: keep.tile([P, part[2] - part[1], 2, SLOT], F32, name="partner%d" % part[1])
+            part: keep.tile(
+                [P, PAD + (part[2] - part[1]) * 2 * SLOT], F32, name="partner%d" % part[1], align_bytes=64
+            )
             for part in last_parts
         }
 
         raw = {}
         grp = {}
         acc = {}
-        halves = {}
 
         def load_rows(n, r0, r1):
             tile = keep.tile([P, PACK, (r1 - r0) * HG], BF16, name="raw%d_%d" % (n, r0))
@@ -118,7 +125,7 @@ def tile_sparseconv2d_t_kernel(tc, x, weight, bias, grad_out, out):
 
         def quantise_chunk(j):
             pair, part = divmod(j, CHUNKS_PER_PAIR)
-            c0 = (PERIOD * pair + LEAD + CHUNK_ROWS * part) * ROW_COLS
+            c0 = (FRONT + PERIOD * pair + LEAD + CHUNK_ROWS * part) * ROW_COLS
             cols = slice(c0, c0 + CHUNK_ROWS * ROW_COLS)
             nc.vector.quantize_mx(
                 out=g_codes[:, cols].bitcast(E5M2_X4),
@@ -126,27 +133,27 @@ def tile_sparseconv2d_t_kernel(tc, x, weight, bias, grad_out, out):
                 in_=grp[j][:].rearrange("p r n q t -> p (r n q t)"),
             )
 
-        def prepare_weights(a, i0):
+        def weight_copy(engine, a, i):
             w_src = w_raw[:].rearrange("p t (c i a b) -> p t c i a b", i=KS, a=2, b=2)
-            nc.vector.tensor_copy(
-                out=w_grp[:, a, i0], in_=w_src[:, :, :, i0, a, :].rearrange("p t c b -> p c b t")
-            )
-            nc.scalar.copy(
-                out=w_grp[:, a, i0 + 1],
-                in_=w_src[:, :, :, i0 + 1, a, :].rearrange("p t c b -> p c b t"),
-            )
+            view = w_src[:, :, :, i, a, :].rearrange("p t c b -> p c b t")
+            if engine == "vector":
+                nc.vector.tensor_copy(out=w_grp[:, a, i], in_=view)
+            else:
+                nc.scalar.copy(out=w_grp[:, a, i], in_=view)
+
+        def weight_quantise(a, i0, n):
             c0 = (a * KS + i0) * P
             nc.vector.quantize_mx(
-                out=w_codes[:, c0 : c0 + 2 * P].bitcast(E4M3_X4),
-                scales=w_scales[:, c0 : c0 + 2 * P],
-                in_=w_grp[:, a, i0 : i0 + 2].rearrange("p i c b t -> p (i c b t)"),
+                out=w_codes[:, c0 : c0 + n * P].bitcast(E4M3_X4),
+                scales=w_scales[:, c0 : c0 + n * P],
+                in_=w_grp[:, a, i0 : i0 + n].rearrange("p i c b t -> p (i c b t)"),
             )
 
         def matmuls(k):
             for a in range(2):
                 acc[k, a] = banks.tile([P, WIN_COLS], F32, name="acc")
                 for i in range(KS):
-                    c0 = WIN_COLS * k + ROW_COLS * (LEAD - i)
+                    c0 = WIN_COLS * k + ROW_COLS * (FRONT + LEAD - i)
                     s0 = (a * KS + i) * P
                     nc.tensor.matmul_mx(
                         out=acc[k, a][:],
@@ -159,7 +166,7 @@ def tile_sparseconv2d_t_kernel(tc, x, weight, bias, grad_out, out):
                     )
 
         def evacuate(k):
-            slot = sums[:, k].rearrange("p n (r w) -> p r n w", w=HX)
+            slot = sums[:, k].rearrange("p n (r w) -> p r n w", w=PITCH)
             for a in range(2):
                 src = acc[k, a][:].rearrange("p (r n q) -> p r n q", n=2, q=HG)
                 dst = slot[:, :, :, 2 * a : 2 * a + HG]
@@ -172,70 +179,93 @@ def tile_sparseconv2d_t_kernel(tc, x, weight, bias, grad_out, out):
             pair, k0, k1 = part
             if part in partner:
                 for b in range(2):
-                    nc.sync.dma_start(out=partner[part][b:P:2], in_=sums[1 - b : P : 2, k0:k1])
-                return
-            halves[part] = [
-                merged.tile([P, k1 - k0, SLOT], F32, name="half%d" % b) for b in range(2)
-            ]
-            for img in range(2):
-                for b in range(2):
                     nc.sync.dma_start(
-                        out=halves[part][b][img:P:2], in_=sums[b:P:2, k0:k1, img, :]
+                        out=partner[part][b:P:2, PAD:],
+                        in_=sums[1 - b : P : 2, k0:k1].rearrange("p k n f -> p (k n f)"),
                     )
+                return
+            for img in range(2):
+                nc.sync.dma_start(
+                    out=half_even[img:P:2, :].rearrange("p (k f) -> p k f", f=SLOT),
+                    in_=sums[0:P:2, k0:k1, img, :],
+                )
+                nc.sync.dma_start(
+                    out=half_odd[img:P:2, PAD:].rearrange("p (k f) -> p k f", f=SLOT),
+                    in_=sums[1:P:2, k0:k1, img, :],
+                )
 
         def finish_merge(part):
             pair, k0, k1 = part
             if part in partner:
-                nc.vector.tensor_tensor(
-                    out=sums[:, k0:k1, :, 1:SLOT],
-                    in0=sums[:, k0:k1, :, 1:SLOT],
-                    in1=partner[part][:, :, :, 0 : SLOT - 1],
-                    op=ADD,
-                )
                 for k in range(k0, k1):
-                    h0, h1, v0 = out_rows(pair, k, k + 1)
+                    h0, h1, row0 = out_rows(pair, k, k + 1)
+                    res = results.tile([P, 2, WIN_ROWS * HX], F32, name="res")
+                    base = PAD - 1 + (k - k0) * 2 * SLOT
+                    nc.vector.tensor_tensor(
+                        out=res[:].rearrange("p n (r w) -> p n r w", w=HX),
+                        in0=sums[:, k].rearrange("p n (r w) -> p n r w", w=PITCH)[:, :, :, 0:HX],
+                        in1=partner[part][:, base : base + 2 * SLOT].rearrange(
+                            "p (n r w) -> p n r w", n=2, w=PITCH
+                        )[:, :, :, 0:HX],
+                        op=ADD,
+                    )
                     nc.sync.dma_start(
                         out=out[2 * pair : 2 * pair + 2].rearrange("n c h w -> c n (h w)")[
                             :, :, h0 * HX : h1 * HX
                         ],
-                        in_=sums[0:P:2, k, :, v0 : v0 + (h1 - h0) * HX],
+                        in_=res[0:P:2, :, row0 * HX : (row0 + h1 - h0) * HX],
                     )
                 return
-            h0, h1, v0 = out_rows(pair, k0, k1)
-            v1 = v0 + (h1 - h0) * HX
-            even, odd = [half[:].rearrange("p s f -> p (s f)") for half in halves[part]]
+            h0, h1, row0 = out_rows(pair, k0, k1)
+            v0 = row0 * PITCH
+            res = results.tile([P, HX * HX], F32, name="res")
             nc.vector.tensor_tensor(
-                out=even[:, v0 + 1 : v1], in0=even[:, v0 + 1 : v1], in1=odd[:, v0 : v1 - 1], op=ADD
+                out=res[:].rearrange("p (h w) -> p h w", w=HX),
+                in0=half_even[:, v0 : v0 + HX * PITCH].rearrange("p (h w) -> p h w", w=PITCH)[
+                    :, :, 0:HX
+                ],
+                in1=half_odd[:, PAD - 1 + v0 : PAD - 1 + v0 + HX * PITCH].rearrange(
+                    "p (h w) -> p h w", w=PITCH
+                )[:, :, 0:HX],
+                op=ADD,
             )
             for img in range(2):
                 nc.sync.dma_start(
-                    out=out[2 * pair + img].rearrange("c h w -> c (h w)"), in_=even[img:P:2, v0:v1]
+                    out=out[2 * pair + img].rearrange("c h w -> c (h w)"), in_=res[img:P:2, :]
                 )
 
-        for n in range(2):
-            load_rows(n, 0, CHUNK_ROWS)
+        for r0 in (0, CHUNK_ROWS):
+            for n in range(2):
+                load_rows(n, r0, r0 + CHUNK_ROWS)
         nc.sync.dma_start(out=w_raw[:], in_=weight.rearrange("(p t) f -> p t f", t=PACK))
         for n in range(2):
-            load_rows(n, CHUNK_ROWS, HALF_ROWS)
-        for n in range(2):
-            load_rows(n, HALF_ROWS, HG)
-        for n in range(2, 4):
-            load_rows(n, 0, HALF_ROWS)
-        for n in range(2, 4):
-            load_rows(n, HALF_ROWS, HG)
+            load_rows(n, 2 * CHUNK_ROWS, HG)
+        for r0 in (0, HG // 2):
+            for n in range(2, 4):
+                load_rows(n, r0, r0 + HG // 2)
         for n in range(4, N_IMG):
             load_rows(n, 0, HG)
 
-        for pair in range(PAIRS + 1):
-            c0 = max(PERIOD * pair - 1, 0) * ROW_COLS
-            c1 = (PERIOD * pair + LEAD) * ROW_COLS
-            nc.vector.memset(g_codes[:, c0:c1].bitcast(I32), 0)
-            nc.vector.memset(g_scales[:, c0:c1].bitcast(I32), 0)
+        group = PERIOD * ROW_COLS
+        zeros = (FRONT + LEAD) * ROW_COLS
+        body = PAIRS * group
+        for plane, per_word in ((g_codes[:].bitcast(I32), 1), (g_scales[:].bitcast(I32), 4)):
+            nc.vector.memset(
+                plane[:, 0 : body // per_word].rearrange("p (g x) -> p g x", x=group // per_word)[
+                    :, :, 0 : zeros // per_word
+                ],
+                0,
+            )
+            nc.vector.memset(plane[:, body // per_word : (body + zeros) // per_word], 0)
         nc.vector.memset(
-            sums[:].rearrange("p k n (r w) -> p (k n r) w", w=HX)[:, :, HG - 1 : HX], 0.0
+            sums[:].rearrange("p k n (r w) -> p (k n r) w", w=PITCH)[:, :, HG:PITCH], 0.0
         )
+        nc.vector.memset(half_odd[:, 0:PAD], 0.0)
+        for part in last_parts:
+            nc.vector.memset(partner[part][:, 0:PAD], 0.0)
 
         copy_chunk(0, SHARES_START)
+        copy_chunk(1, SHARES_START)
         warm = banks.tile([P, WIN_COLS], F32, name="acc")
         warm_src = raw[0, 0].rearrange("p t x -> p (t x)")
         for w_i in range(WARM_UP):
@@ -243,14 +273,26 @@ def tile_sparseconv2d_t_kernel(tc, x, weight, bias, grad_out, out):
                 out=warm[:], lhsT=warm_src[:, 0:P], rhs=warm_src[:, 0:WIN_COLS], start=True, stop=True
             )
         quantise_chunk(0)
-        for a in range(2):
-            for i0 in range(0, KS, 2):
-                prepare_weights(a, i0)
-        copy_chunk(1, SHARES_START)
         quantise_chunk(1)
+        weight_copy("vector", 0, 0)
+        weight_copy("scalar", 0, 1)
+        weight_copy("vector", 0, 2)
+        weight_copy("scalar", 0, 3)
+        weight_quantise(0, 0, 1)
+        weight_quantise(0, 1, 1)
+        weight_copy("vector", 1, 0)
+        weight_copy("scalar", 1, 1)
+        weight_quantise(0, 2, 2)
+        weight_copy("vector", 1, 2)
+        weight_copy("scalar", 1, 3)
+        weight_quantise(1, 0, 2)
+        weight_quantise(1, 2, 2)
         copy_chunk(2, SHARES)
 
         for k in range(N_WIN + MERGE_LAG):
+            for part in parts:
+                if part[2] - 1 == k - MERGE_LAG:
+                    finish_merge(part)
             if k + COPY_AHEAD < N_CHUNKS:
                 copy_chunk(k + COPY_AHEAD, SHARES)
             if k + QUANT_AHEAD < N_CHUNKS:
@@ -261,6 +303,3 @@ def tile_sparseconv2d_t_kernel(tc, x, weight, bias, grad_out, out):
             for part in parts:
                 if part[2] - 1 == k:
                     start_merge(part)
-            for part in parts:
-                if part[2] - 1 == k - MERGE_LAG:
-                    finish_merge(part)

@@ -290,9 +290,6 @@ def tile_sparseconv2d_t_kernel(tc, x, weight, bias, grad_out, out):
         copy_chunk(2, SHARES)
 
         for k in range(N_WIN + MERGE_LAG):
-            for part in parts:
-                if part[2] - 1 == k - MERGE_LAG:
-                    finish_merge(part)
             if k + COPY_AHEAD < N_CHUNKS:
                 copy_chunk(k + COPY_AHEAD, SHARES)
             if k + QUANT_AHEAD < N_CHUNKS:
@@ -303,3 +300,6 @@ def tile_sparseconv2d_t_kernel(tc, x, weight, bias, grad_out, out):
             for part in parts:
                 if part[2] - 1 == k:
                     start_merge(part)
+            for part in parts:
+                if part[2] - 1 == k - MERGE_LAG:
+                    finish_merge(part)

@@ -149,21 +149,23 @@ def tile_sparseconv2d_t_kernel(tc, x, weight, bias, grad_out, out):
                 in_=w_grp[:, a, i0 : i0 + n].rearrange("p i c b t -> p (i c b t)"),
             )
 
-        def matmuls(k):
+        def matmuls(wins):
             for a in range(2):
-                acc[k, a] = banks.tile([P, WIN_COLS], F32, name="acc")
+                for k in wins:
+                    acc[k, a] = banks.tile([P, WIN_COLS], F32, name="acc")
                 for i in range(KS):
-                    c0 = WIN_COLS * k + ROW_COLS * (FRONT + LEAD - i)
                     s0 = (a * KS + i) * P
-                    nc.tensor.matmul_mx(
-                        out=acc[k, a][:],
-                        lhsT=w_codes[:, s0 : s0 + P].bitcast(E4M3_X4),
-                        lhsT_scale=w_scales[:, s0 : s0 + P],
-                        rhs=g_codes[:, c0 : c0 + WIN_COLS].bitcast(E5M2_X4),
-                        rhs_scale=g_scales[:, c0 : c0 + WIN_COLS],
-                        start=(i == 0),
-                        stop=(i == KS - 1),
-                    )
+                    for k in wins:
+                        c0 = WIN_COLS * k + ROW_COLS * (FRONT + LEAD - i)
+                        nc.tensor.matmul_mx(
+                            out=acc[k, a][:],
+                            lhsT=w_codes[:, s0 : s0 + P].bitcast(E4M3_X4),
+                            lhsT_scale=w_scales[:, s0 : s0 + P],
+                            rhs=g_codes[:, c0 : c0 + WIN_COLS].bitcast(E5M2_X4),
+                            rhs_scale=g_scales[:, c0 : c0 + WIN_COLS],
+                            start=(i == 0),
+                            stop=(i == KS - 1),
+                        )
 
         def evacuate(k):
             slot = sums[:, k].rearrange("p n (r w) -> p r n w", w=PITCH)
@@ -289,17 +291,26 @@ def tile_sparseconv2d_t_kernel(tc, x, weight, bias, grad_out, out):
         weight_quantise(1, 2, 2)
         copy_chunk(2, SHARES)
 
+        started = {}
         for k in range(N_WIN + MERGE_LAG):
             if k + COPY_AHEAD < N_CHUNKS:
                 copy_chunk(k + COPY_AHEAD, SHARES)
             if k + QUANT_AHEAD < N_CHUNKS:
                 quantise_chunk(k + QUANT_AHEAD)
-            if k < N_WIN:
-                matmuls(k)
-                evacuate(k)
+            wins = []
+            if k < N_WIN - 2:
+                if k % 2 == 1:
+                    wins = [k - 1, k]
+            elif k < N_WIN:
+                wins = [k]
+            if wins:
+                matmuls(wins)
+            for kk in wins:
+                evacuate(kk)
             for part in parts:
-                if part[2] - 1 == k:
+                if part[2] - 1 in wins:
                     start_merge(part)
+                    started[part] = k
             for part in parts:
-                if part[2] - 1 == k - MERGE_LAG:
+                if started.get(part, k) == k - MERGE_LAG:
                     finish_merge(part)

@@ -40,6 +40,8 @@ SHARES = (("vector", 0, 0, 4), ("gpsimd", 0, 4, 8), ("scalar", 1, 0, 8))
 COPY_AHEAD, QUANT_AHEAD = 3, 2
 MERGE_LAG = 2
 WARM_UP = 8
+F_LEN = C * KS * KS
+EXTRA_FROM = 2
 
 FLOPS = 2 * CO * C * KS * KS * N_IMG * HG * HG
 BYTES = CO * C * KS * KS * 2 + N_IMG * CO * HG * HG * 2 + N_IMG * C * HX * HX * 4
@@ -62,7 +64,10 @@ def tile_sparseconv2d_t_kernel(tc, x, weight, bias, grad_out, out):
 
         g_codes = keep.tile([P, PLANE_COLS], U32, align_bytes=64)
         g_scales = keep.tile([P, PLANE_COLS], U8, align_bytes=64)
-        w_raw = keep.tile([P, PACK, C * KS * KS], BF16)
+        w_raw = keep.tile([P, PACK * F_LEN + KS * KS], BF16)
+        x_codes = keep.tile([P, 2 * KS * P], U32, align_bytes=64)
+        x_scales = keep.tile([P, 2 * KS * P], U8, align_bytes=64)
+        final = keep.tile([P, 2, WIN_ROWS * HX], F32, align_bytes=64)
         w_grp = keep.tile([P, 2, KS, C, 2, PACK], BF16, align_bytes=64)
         w_codes = keep.tile([P, 2 * KS * P], U32, align_bytes=64)
         w_scales = keep.tile([P, 2 * KS * P], U8, align_bytes=64)
@@ -74,11 +79,7 @@ def tile_sparseconv2d_t_kernel(tc, x, weight, bias, grad_out, out):
         for pair in range(PAIRS - 1):
             k0 = PERIOD * pair // WIN_ROWS
             parts.append((pair, k0, k0 + PAIR_WINS))
-        last_parts = [
-            (PAIRS - 1, N_WIN - PAIR_WINS, N_WIN - 2),
-            (PAIRS - 1, N_WIN - 2, N_WIN - 1),
-            (PAIRS - 1, N_WIN - 1, N_WIN),
-        ]
+        last_parts = [(PAIRS - 1, k, k + 1) for k in range(N_WIN - PAIR_WINS, N_WIN - 1)]
         parts.extend(last_parts)
         partner = {
             part: keep.tile(
@@ -134,12 +135,34 @@ def tile_sparseconv2d_t_kernel(tc, x, weight, bias, grad_out, out):
             )
 
         def weight_copy(engine, a, i):
-            w_src = w_raw[:].rearrange("p t (c i a b) -> p t c i a b", i=KS, a=2, b=2)
+            w_src = w_raw[:, 0 : PACK * F_LEN].rearrange(
+                "p (t c i a b) -> p t c i a b", t=PACK, i=KS, a=2, b=2
+            )
             view = w_src[:, :, :, i, a, :].rearrange("p t c b -> p c b t")
             if engine == "vector":
                 nc.vector.tensor_copy(out=w_grp[:, a, i], in_=view)
             else:
                 nc.scalar.copy(out=w_grp[:, a, i], in_=view)
+
+        def extra_copy(engine, half, i):
+            f0 = KS * i + 2 * half + 1
+            view = (
+                w_raw[:, f0 : f0 + PACK * F_LEN]
+                .rearrange("p (t c x) -> p t c x", t=PACK, x=KS * KS)[:, :, :, 0:2]
+                .rearrange("p t c b -> p c b t")
+            )
+            if engine == "vector":
+                nc.vector.tensor_copy(out=w_grp[:, half, i], in_=view)
+            else:
+                nc.scalar.copy(out=w_grp[:, half, i], in_=view)
+
+        def extra_quantise(half):
+            c0 = half * KS * P
+            nc.vector.quantize_mx(
+                out=x_codes[:, c0 : c0 + KS * P].bitcast(E4M3_X4),
+                scales=x_scales[:, c0 : c0 + KS * P],
+                in_=w_grp[:, half].rearrange("p i c b t -> p (i c b t)"),
+            )
 
         def weight_quantise(a, i0, n):
             c0 = (a * KS + i0) * P
@@ -177,6 +200,36 @@ def tile_sparseconv2d_t_kernel(tc, x, weight, bias, grad_out, out):
                 else:
                     nc.vector.tensor_tensor(out=dst, in0=src, in1=dst, op=ADD)
 
+        def last_window():
+            k = N_WIN - 1
+            rows = final[:].rearrange("p n (r w) -> p r n w", w=HX)
+            for s in range(KS):
+                bank = banks.tile([P, WIN_COLS], F32, name="acc")
+                codes, scales = (w_codes, w_scales) if s % 2 == 0 else (x_codes, x_scales)
+                for i in range(KS):
+                    c0 = WIN_COLS * k + ROW_COLS * (FRONT + LEAD - i)
+                    s0 = ((s // 2) * KS + i) * P
+                    nc.tensor.matmul_mx(
+                        out=bank[:],
+                        lhsT=codes[:, s0 : s0 + P].bitcast(E4M3_X4),
+                        lhsT_scale=scales[:, s0 : s0 + P],
+                        rhs=g_codes[:, c0 : c0 + WIN_COLS].bitcast(E5M2_X4),
+                        rhs_scale=g_scales[:, c0 : c0 + WIN_COLS],
+                        start=(i == 0),
+                        stop=(i == KS - 1),
+                    )
+                src = bank[:].rearrange("p (r n q) -> p r n q", n=2, q=HG)
+                dst = rows[:, :, :, s : s + HG]
+                if s == 0:
+                    nc.scalar.copy(out=dst, in_=src)
+                else:
+                    nc.vector.tensor_tensor(out=dst, in0=src, in1=dst, op=ADD)
+            h0, h1, row0 = out_rows(PAIRS - 1, k, k + 1)
+            nc.scalar.dma_start(
+                out=out[N_IMG - 2 : N_IMG].rearrange("n c h w -> c n (h w)")[:, :, h0 * HX : h1 * HX],
+                in_=final[0:P:2, :, row0 * HX : (row0 + h1 - h0) * HX],
+            )
+
         def start_merge(part):
             pair, k0, k1 = part
             if part in partner:
@@ -196,14 +249,15 @@ def tile_sparseconv2d_t_kernel(tc, x, weight, bias, grad_out, out):
                     in_=sums[1:P:2, k0:k1, img, :],
                 )
 
-        def finish_merge(part):
+        def finish_merge(part, engine):
             pair, k0, k1 = part
+            adder = nc.gpsimd if engine == "gpsimd" else nc.vector
             if part in partner:
                 for k in range(k0, k1):
                     h0, h1, row0 = out_rows(pair, k, k + 1)
                     res = results.tile([P, 2, WIN_ROWS * HX], F32, name="res")
                     base = PAD - 1 + (k - k0) * 2 * SLOT
-                    nc.vector.tensor_tensor(
+                    adder.tensor_tensor(
                         out=res[:].rearrange("p n (r w) -> p n r w", w=HX),
                         in0=sums[:, k].rearrange("p n (r w) -> p n r w", w=PITCH)[:, :, :, 0:HX],
                         in1=partner[part][:, base : base + 2 * SLOT].rearrange(
@@ -239,7 +293,10 @@ def tile_sparseconv2d_t_kernel(tc, x, weight, bias, grad_out, out):
         for r0 in (0, CHUNK_ROWS):
             for n in range(2):
                 load_rows(n, r0, r0 + CHUNK_ROWS)
-        nc.sync.dma_start(out=w_raw[:], in_=weight.rearrange("(p t) f -> p t f", t=PACK))
+        nc.sync.dma_start(
+            out=w_raw[:, 0 : PACK * F_LEN].rearrange("p (t f) -> p t f", t=PACK),
+            in_=weight.rearrange("(p t) f -> p t f", t=PACK),
+        )
         for n in range(2):
             load_rows(n, 2 * CHUNK_ROWS, HG)
         for r0 in (0, HG // 2):
@@ -262,6 +319,8 @@ def tile_sparseconv2d_t_kernel(tc, x, weight, bias, grad_out, out):
         nc.vector.memset(
             sums[:].rearrange("p k n (r w) -> p (k n r) w", w=PITCH)[:, :, HG:PITCH], 0.0
         )
+        nc.vector.memset(w_raw[:, PACK * F_LEN : PACK * F_LEN + KS * KS], 0.0)
+        nc.vector.memset(final[:].rearrange("p n (r w) -> p (n r) w", w=HX)[:, :, HG:HX], 0.0)
         nc.vector.memset(half_odd[:, 0:PAD], 0.0)
         for part in last_parts:
             nc.vector.memset(partner[part][:, 0:PAD], 0.0)
@@ -292,13 +351,28 @@ def tile_sparseconv2d_t_kernel(tc, x, weight, bias, grad_out, out):
         copy_chunk(2, SHARES)
 
         started = {}
+
+        def finishes(k, engine):
+            for part in parts:
+                if started.get(part, k) == k - MERGE_LAG:
+                    finish_merge(part, engine)
+
         for k in range(N_WIN + MERGE_LAG):
             if k + COPY_AHEAD < N_CHUNKS:
                 copy_chunk(k + COPY_AHEAD, SHARES)
             if k + QUANT_AHEAD < N_CHUNKS:
                 quantise_chunk(k + QUANT_AHEAD)
+            if EXTRA_FROM <= k < EXTRA_FROM + 2 * KS:
+                half, i = divmod(k - EXTRA_FROM, KS)
+                extra_copy("vector" if i % 2 == 0 else "scalar", half, i)
+            if k == EXTRA_FROM + KS or k == EXTRA_FROM + 2 * KS:
+                extra_quantise((k - EXTRA_FROM) // KS - 1)
+            if k == N_WIN - 1:
+                last_window()
+                finishes(k, "gpsimd")
+                continue
             wins = []
-            if k < N_WIN - 2:
+            if k < N_WIN - PAIR_WINS + 1:
                 if k % 2 == 1:
                     wins = [k - 1, k]
             elif k < N_WIN:
@@ -311,6 +385,4 @@ def tile_sparseconv2d_t_kernel(tc, x, weight, bias, grad_out, out):
                 if part[2] - 1 in wins:
                     start_merge(part)
                     started[part] = k
-            for part in parts:
-                if started.get(part, k) == k - MERGE_LAG:
-                    finish_merge(part)
+            finishes(k, "gpsimd" if k >= N_WIN else "vector")

@@ -89,6 +89,7 @@ def tile_sparseconv2d_t_kernel(tc, x, weight, bias, grad_out, out):
         }
 
         raw = {}
+        whole = {}
         grp = {}
         acc = {}
 
@@ -98,6 +99,7 @@ def tile_sparseconv2d_t_kernel(tc, x, weight, bias, grad_out, out):
                 out=tile[:],
                 in_=grad_out[n, :, r0:r1, :].rearrange("(p t) h w -> p t (h w)", t=PACK),
             )
+            whole[n, r0] = tile
             for r in range(r0, r1, CHUNK_ROWS):
                 raw[n, r] = tile[:, :, (r - r0) * HG : (r - r0 + CHUNK_ROWS) * HG]
 
@@ -290,9 +292,8 @@ def tile_sparseconv2d_t_kernel(tc, x, weight, bias, grad_out, out):
                     out=out[2 * pair + img].rearrange("c h w -> c (h w)"), in_=res[img:P:2, :]
                 )
 
-        for r0 in (0, CHUNK_ROWS):
-            for n in range(2):
-                load_rows(n, r0, r0 + CHUNK_ROWS)
+        for n in range(2):
+            load_rows(n, 0, 2 * CHUNK_ROWS)
         nc.sync.dma_start(
             out=w_raw[:, 0 : PACK * F_LEN].rearrange("p (t f) -> p t f", t=PACK),
             in_=weight.rearrange("(p t) f -> p t f", t=PACK),
@@ -328,10 +329,13 @@ def tile_sparseconv2d_t_kernel(tc, x, weight, bias, grad_out, out):
         copy_chunk(0, SHARES_START)
         copy_chunk(1, SHARES_START)
         warm = banks.tile([P, WIN_COLS], F32, name="acc")
-        warm_src = raw[0, 0].rearrange("p t x -> p (t x)")
         for w_i in range(WARM_UP):
             nc.tensor.matmul(
-                out=warm[:], lhsT=warm_src[:, 0:P], rhs=warm_src[:, 0:WIN_COLS], start=True, stop=True
+                out=warm[:],
+                lhsT=whole[0, 0][:, 0, 0:P],
+                rhs=whole[0, 0][:, 1, 0:WIN_COLS],
+                start=True,
+                stop=True,
             )
         quantise_chunk(0)
         quantise_chunk(1)

@@ -41,7 +41,7 @@ COPY_AHEAD, QUANT_AHEAD = 3, 2
 MERGE_LAG = 2
 WARM_UP = 8
 F_LEN = C * KS * KS
-EXTRA_FROM = 2
+SHIFT_AT = 13
 
 FLOPS = 2 * CO * C * KS * KS * N_IMG * HG * HG
 BYTES = CO * C * KS * KS * 2 + N_IMG * CO * HG * HG * 2 + N_IMG * C * HX * HX * 4
@@ -64,7 +64,7 @@ def tile_sparseconv2d_t_kernel(tc, x, weight, bias, grad_out, out):
 
         g_codes = keep.tile([P, PLANE_COLS], U32, align_bytes=64)
         g_scales = keep.tile([P, PLANE_COLS], U8, align_bytes=64)
-        w_raw = keep.tile([P, PACK * F_LEN + KS * KS], BF16)
+        w_raw = keep.tile([P, PACK * F_LEN], BF16)
         x_codes = keep.tile([P, 2 * KS * P], U32, align_bytes=64)
         x_scales = keep.tile([P, 2 * KS * P], U8, align_bytes=64)
         final = keep.tile([P, 2, WIN_ROWS * HX], F32, align_bytes=64)
@@ -137,7 +137,7 @@ def tile_sparseconv2d_t_kernel(tc, x, weight, bias, grad_out, out):
             )
 
         def weight_copy(engine, a, i):
-            w_src = w_raw[:, 0 : PACK * F_LEN].rearrange(
+            w_src = w_raw[:].rearrange(
                 "p (t c i a b) -> p t c i a b", t=PACK, i=KS, a=2, b=2
             )
             view = w_src[:, :, :, i, a, :].rearrange("p t c b -> p c b t")
@@ -146,25 +146,13 @@ def tile_sparseconv2d_t_kernel(tc, x, weight, bias, grad_out, out):
             else:
                 nc.scalar.copy(out=w_grp[:, a, i], in_=view)
 
-        def extra_copy(engine, half, i):
-            f0 = KS * i + 2 * half + 1
-            view = (
-                w_raw[:, f0 : f0 + PACK * F_LEN]
-                .rearrange("p (t c x) -> p t c x", t=PACK, x=KS * KS)[:, :, :, 0:2]
-                .rearrange("p t c b -> p c b t")
-            )
-            if engine == "vector":
-                nc.vector.tensor_copy(out=w_grp[:, half, i], in_=view)
-            else:
-                nc.scalar.copy(out=w_grp[:, half, i], in_=view)
+        def shift_codes():
+            n = 2 * KS * P - 1
+            nc.vector.tensor_copy(out=x_codes[:, 0:n].bitcast(I32), in_=w_codes[:, 1 : n + 1].bitcast(I32))
 
-        def extra_quantise(half):
-            c0 = half * KS * P
-            nc.vector.quantize_mx(
-                out=x_codes[:, c0 : c0 + KS * P].bitcast(E4M3_X4),
-                scales=x_scales[:, c0 : c0 + KS * P],
-                in_=w_grp[:, half].rearrange("p i c b t -> p (i c b t)"),
-            )
+        def shift_scales():
+            n = 2 * KS * P - 1
+            nc.vector.tensor_copy(out=x_scales[:, 0:n], in_=w_scales[:, 1 : n + 1])
 
         def weight_quantise(a, i0, n):
             c0 = (a * KS + i0) * P
@@ -295,7 +283,7 @@ def tile_sparseconv2d_t_kernel(tc, x, weight, bias, grad_out, out):
         for n in range(2):
             load_rows(n, 0, 2 * CHUNK_ROWS)
         nc.sync.dma_start(
-            out=w_raw[:, 0 : PACK * F_LEN].rearrange("p (t f) -> p t f", t=PACK),
+            out=w_raw[:].rearrange("p (t f) -> p t f", t=PACK),
             in_=weight.rearrange("(p t) f -> p t f", t=PACK),
         )
         for n in range(2):
@@ -320,7 +308,8 @@ def tile_sparseconv2d_t_kernel(tc, x, weight, bias, grad_out, out):
         nc.vector.memset(
             sums[:].rearrange("p k n (r w) -> p (k n r) w", w=PITCH)[:, :, HG:PITCH], 0.0
         )
-        nc.vector.memset(w_raw[:, PACK * F_LEN : PACK * F_LEN + KS * KS], 0.0)
+        nc.vector.memset(x_codes[:, 2 * KS * P - 1 :].bitcast(I32), 0)
+        nc.vector.memset(x_scales[:, 2 * KS * P - 4 :].bitcast(I32), 0)
         nc.vector.memset(final[:].rearrange("p n (r w) -> p (n r) w", w=HX)[:, :, HG:HX], 0.0)
         nc.vector.memset(half_odd[:, 0:PAD], 0.0)
         for part in last_parts:
@@ -366,11 +355,10 @@ def tile_sparseconv2d_t_kernel(tc, x, weight, bias, grad_out, out):
                 copy_chunk(k + COPY_AHEAD, SHARES)
             if k + QUANT_AHEAD < N_CHUNKS:
                 quantise_chunk(k + QUANT_AHEAD)
-            if EXTRA_FROM <= k < EXTRA_FROM + 2 * KS:
-                half, i = divmod(k - EXTRA_FROM, KS)
-                extra_copy("vector" if i % 2 == 0 else "scalar", half, i)
-            if k == EXTRA_FROM + KS or k == EXTRA_FROM + 2 * KS:
-                extra_quantise((k - EXTRA_FROM) // KS - 1)
+            if k == SHIFT_AT:
+                shift_codes()
+            if k == SHIFT_AT + 1:
+                shift_scales()
             if k == N_WIN - 1:
                 last_window()
                 finishes(k, "gpsimd")

@@ -21,36 +21,42 @@ HX = HG + KS - 1
 PAIRS = N_IMG // 2
 ROW_COLS = 2 * HG
 LEAD = KS - 1
-PERIOD = LEAD + HG + 1
-FRONT = 1
+PERIOD = HG + LEAD
 WIN_ROWS = 8
 WIN_COLS = WIN_ROWS * ROW_COLS
-N_WIN = PAIRS * PERIOD // WIN_ROWS
-PLANE_ROWS = FRONT + PAIRS * PERIOD + LEAD
+OUT_ROWS = PAIRS * PERIOD
+N_WIN = -(-OUT_ROWS // WIN_ROWS)
+LAST_ROWS = OUT_ROWS - (N_WIN - 1) * WIN_ROWS
+PLANE_ROWS = LEAD + N_WIN * WIN_ROWS
 PLANE_COLS = PLANE_ROWS * ROW_COLS
 CHUNK_ROWS = 8
 CHUNKS_PER_PAIR = HG // CHUNK_ROWS
 N_CHUNKS = PAIRS * CHUNKS_PER_PAIR
-PAIR_WINS = 5
+UNIT = 2
 PITCH = 36
 SLOT = WIN_ROWS * PITCH
 PAD = 4
 SHARES_START = (("vector", 0, 0, 8), ("scalar", 1, 0, 4), ("gpsimd", 1, 4, 8))
 SHARES = (("vector", 0, 0, 4), ("gpsimd", 0, 4, 8), ("scalar", 1, 0, 8))
 COPY_AHEAD, QUANT_AHEAD = 3, 2
-MERGE_LAG = 2
+MERGE_LAG = 4
+MERGE_SETS = 3
 WARM_UP = 8
+SHIFT_AT = 3
 F_LEN = C * KS * KS
-SHIFT_AT = 13
+SHIFT_AT = 3
 
 FLOPS = 2 * CO * C * KS * KS * N_IMG * HG * HG
 BYTES = CO * C * KS * KS * 2 + N_IMG * CO * HG * HG * 2 + N_IMG * C * HX * HX * 4
 
 
-def out_rows(pair, k0, k1):
-    h0 = max(WIN_ROWS * k0 - PERIOD * pair, 0)
-    h1 = min(WIN_ROWS * k1 - PERIOD * pair, HX)
-    return h0, h1, PERIOD * pair + h0 - WIN_ROWS * k0
+def segments(r0, r1):
+    found = []
+    for pair in range(PAIRS):
+        a, b = max(r0, PERIOD * pair), min(r1, PERIOD * (pair + 1))
+        if a < b:
+            found.append((pair, a - PERIOD * pair, b - PERIOD * pair, a - r0))
+    return found
 
 
 def tile_sparseconv2d_t_kernel(tc, x, weight, bias, grad_out, out):
@@ -58,7 +64,7 @@ def tile_sparseconv2d_t_kernel(tc, x, weight, bias, grad_out, out):
     with ExitStack() as ctx:
         keep = ctx.enter_context(tc.tile_pool(name="keep", bufs=1))
         grouped = ctx.enter_context(tc.tile_pool(name="grouped", bufs=4))
-        results = ctx.enter_context(tc.tile_pool(name="results", bufs=3))
+        results = ctx.enter_context(tc.tile_pool(name="results", bufs=4))
         banks = ctx.enter_context(tc.psum_pool(name="banks", bufs=8))
         ctx.enter_context(tc.manual_schedule())
 
@@ -67,26 +73,18 @@ def tile_sparseconv2d_t_kernel(tc, x, weight, bias, grad_out, out):
         w_raw = keep.tile([P, PACK * F_LEN], BF16)
         x_codes = keep.tile([P, 2 * KS * P], U32, align_bytes=64)
         x_scales = keep.tile([P, 2 * KS * P], U8, align_bytes=64)
-        final = keep.tile([P, 2, WIN_ROWS * HX], F32, align_bytes=64)
+        final = keep.tile([P, 2, LAST_ROWS * HX], F32, align_bytes=64)
         w_grp = keep.tile([P, 2, KS, C, 2, PACK], BF16, align_bytes=64)
         w_codes = keep.tile([P, 2 * KS * P], U32, align_bytes=64)
         w_scales = keep.tile([P, 2 * KS * P], U8, align_bytes=64)
-        sums = keep.tile([P, N_WIN, 2, SLOT], F32, align_bytes=64)
-        half_even = keep.tile([P, PAIR_WINS * SLOT], F32, align_bytes=64)
-        half_odd = keep.tile([P, PAD + PAIR_WINS * SLOT], F32, align_bytes=64)
-
-        parts = []
-        for pair in range(PAIRS - 1):
-            k0 = PERIOD * pair // WIN_ROWS
-            parts.append((pair, k0, k0 + PAIR_WINS))
-        last_parts = [(PAIRS - 1, k, k + 1) for k in range(N_WIN - PAIR_WINS, N_WIN - 1)]
-        parts.extend(last_parts)
-        partner = {
-            part: keep.tile(
-                [P, PAD + (part[2] - part[1]) * 2 * SLOT], F32, name="partner%d" % part[1], align_bytes=64
-            )
-            for part in last_parts
-        }
+        sums = keep.tile([P, N_WIN - 1, 2, SLOT], F32, align_bytes=64)
+        half_even = [
+            keep.tile([P, UNIT * SLOT], F32, name="even%d" % n, align_bytes=64) for n in range(MERGE_SETS)
+        ]
+        half_odd = [
+            keep.tile([P, PAD + UNIT * SLOT], F32, name="odd%d" % n, align_bytes=64) for n in range(MERGE_SETS)
+        ]
+        partner = keep.tile([P, PAD + 2 * SLOT], F32, align_bytes=64)
 
         raw = {}
         whole = {}
@@ -128,7 +126,7 @@ def tile_sparseconv2d_t_kernel(tc, x, weight, bias, grad_out, out):
 
         def quantise_chunk(j):
             pair, part = divmod(j, CHUNKS_PER_PAIR)
-            c0 = (FRONT + PERIOD * pair + LEAD + CHUNK_ROWS * part) * ROW_COLS
+            c0 = (LEAD + PERIOD * pair + CHUNK_ROWS * part) * ROW_COLS
             cols = slice(c0, c0 + CHUNK_ROWS * ROW_COLS)
             nc.vector.quantize_mx(
                 out=g_codes[:, cols].bitcast(E5M2_X4),
@@ -169,7 +167,7 @@ def tile_sparseconv2d_t_kernel(tc, x, weight, bias, grad_out, out):
                 for i in range(KS):
                     s0 = (a * KS + i) * P
                     for k in wins:
-                        c0 = WIN_COLS * k + ROW_COLS * (FRONT + LEAD - i)
+                        c0 = WIN_COLS * k + ROW_COLS * (LEAD - i)
                         nc.tensor.matmul_mx(
                             out=acc[k, a][:],
                             lhsT=w_codes[:, s0 : s0 + P].bitcast(E4M3_X4),
@@ -190,95 +188,83 @@ def tile_sparseconv2d_t_kernel(tc, x, weight, bias, grad_out, out):
                 else:
                     nc.vector.tensor_tensor(out=dst, in0=src, in1=dst, op=ADD)
 
-        def last_window():
+        def last_group(s):
             k = N_WIN - 1
-            rows = final[:].rearrange("p n (r w) -> p r n w", w=HX)
-            for s in range(KS):
-                bank = banks.tile([P, WIN_COLS], F32, name="acc")
-                codes, scales = (w_codes, w_scales) if s % 2 == 0 else (x_codes, x_scales)
-                for i in range(KS):
-                    c0 = WIN_COLS * k + ROW_COLS * (FRONT + LEAD - i)
-                    s0 = ((s // 2) * KS + i) * P
-                    nc.tensor.matmul_mx(
-                        out=bank[:],
-                        lhsT=codes[:, s0 : s0 + P].bitcast(E4M3_X4),
-                        lhsT_scale=scales[:, s0 : s0 + P],
-                        rhs=g_codes[:, c0 : c0 + WIN_COLS].bitcast(E5M2_X4),
-                        rhs_scale=g_scales[:, c0 : c0 + WIN_COLS],
-                        start=(i == 0),
-                        stop=(i == KS - 1),
-                    )
-                src = bank[:].rearrange("p (r n q) -> p r n q", n=2, q=HG)
-                dst = rows[:, :, :, s : s + HG]
-                if s == 0:
-                    nc.scalar.copy(out=dst, in_=src)
-                else:
-                    nc.vector.tensor_tensor(out=dst, in0=src, in1=dst, op=ADD)
-            h0, h1, row0 = out_rows(PAIRS - 1, k, k + 1)
-            nc.scalar.dma_start(
-                out=out[N_IMG - 2 : N_IMG].rearrange("n c h w -> c n (h w)")[:, :, h0 * HX : h1 * HX],
-                in_=final[0:P:2, :, row0 * HX : (row0 + h1 - h0) * HX],
-            )
+            acc[k, s] = banks.tile([P, WIN_COLS], F32, name="acc")
+            codes, scales = (w_codes, w_scales) if s % 2 == 0 else (x_codes, x_scales)
+            for i in range(KS):
+                c0 = WIN_COLS * k + ROW_COLS * (LEAD - i)
+                s0 = ((s // 2) * KS + i) * P
+                nc.tensor.matmul_mx(
+                    out=acc[k, s][:],
+                    lhsT=codes[:, s0 : s0 + P].bitcast(E4M3_X4),
+                    lhsT_scale=scales[:, s0 : s0 + P],
+                    rhs=g_codes[:, c0 : c0 + WIN_COLS].bitcast(E5M2_X4),
+                    rhs_scale=g_scales[:, c0 : c0 + WIN_COLS],
+                    start=(i == 0),
+                    stop=(i == KS - 1),
+                )
 
-        def start_merge(part):
-            pair, k0, k1 = part
-            if part in partner:
-                for b in range(2):
-                    nc.sync.dma_start(
-                        out=partner[part][b:P:2, PAD:],
-                        in_=sums[1 - b : P : 2, k0:k1].rearrange("p k n f -> p (k n f)"),
-                    )
-                return
+        def last_sum(s):
+            src = acc[N_WIN - 1, s][:, 0 : LAST_ROWS * ROW_COLS].rearrange("p (r n q) -> p r n q", n=2, q=HG)
+            dst = final[:].rearrange("p n (r w) -> p r n w", w=HX)[:, :, :, s : s + HG]
+            if s == 0:
+                nc.scalar.copy(out=dst, in_=src)
+            else:
+                nc.vector.tensor_tensor(out=dst, in0=src, in1=dst, op=ADD)
+
+        def store_pair(engine, tile, r0, r1):
+            for pair, h0, h1, at in segments(r0, r1):
+                engine.dma_start(
+                    out=out[2 * pair : 2 * pair + 2].rearrange("n c h w -> c n (h w)")[:, :, h0 * HX : h1 * HX],
+                    in_=tile[0:P:2, :, at * HX : (at + h1 - h0) * HX],
+                )
+
+        def start_merge(u):
             for img in range(2):
                 nc.sync.dma_start(
-                    out=half_even[img:P:2, :].rearrange("p (k f) -> p k f", f=SLOT),
-                    in_=sums[0:P:2, k0:k1, img, :],
+                    out=half_even[u % MERGE_SETS][img:P:2, :].rearrange("p (k f) -> p k f", f=SLOT),
+                    in_=sums[0:P:2, UNIT * u : UNIT * (u + 1), img, :],
                 )
                 nc.sync.dma_start(
-                    out=half_odd[img:P:2, PAD:].rearrange("p (k f) -> p k f", f=SLOT),
-                    in_=sums[1:P:2, k0:k1, img, :],
+                    out=half_odd[u % MERGE_SETS][img:P:2, PAD:].rearrange("p (k f) -> p k f", f=SLOT),
+                    in_=sums[1:P:2, UNIT * u : UNIT * (u + 1), img, :],
                 )
 
-        def finish_merge(part, engine):
-            pair, k0, k1 = part
-            adder = nc.gpsimd if engine == "gpsimd" else nc.vector
-            if part in partner:
-                for k in range(k0, k1):
-                    h0, h1, row0 = out_rows(pair, k, k + 1)
-                    res = results.tile([P, 2, WIN_ROWS * HX], F32, name="res")
-                    base = PAD - 1 + (k - k0) * 2 * SLOT
-                    adder.tensor_tensor(
-                        out=res[:].rearrange("p n (r w) -> p n r w", w=HX),
-                        in0=sums[:, k].rearrange("p n (r w) -> p n r w", w=PITCH)[:, :, :, 0:HX],
-                        in1=partner[part][:, base : base + 2 * SLOT].rearrange(
-                            "p (n r w) -> p n r w", n=2, w=PITCH
-                        )[:, :, :, 0:HX],
-                        op=ADD,
-                    )
-                    nc.sync.dma_start(
-                        out=out[2 * pair : 2 * pair + 2].rearrange("n c h w -> c n (h w)")[
-                            :, :, h0 * HX : h1 * HX
-                        ],
-                        in_=res[0:P:2, :, row0 * HX : (row0 + h1 - h0) * HX],
-                    )
-                return
-            h0, h1, row0 = out_rows(pair, k0, k1)
-            v0 = row0 * PITCH
-            res = results.tile([P, HX * HX], F32, name="res")
+        def finish_merge(u):
+            n = UNIT * WIN_ROWS
+            res = results.tile([P, n * HX], F32, name="res")
             nc.vector.tensor_tensor(
                 out=res[:].rearrange("p (h w) -> p h w", w=HX),
-                in0=half_even[:, v0 : v0 + HX * PITCH].rearrange("p (h w) -> p h w", w=PITCH)[
-                    :, :, 0:HX
-                ],
-                in1=half_odd[:, PAD - 1 + v0 : PAD - 1 + v0 + HX * PITCH].rearrange(
+                in0=half_even[u % MERGE_SETS][:].rearrange("p (h w) -> p h w", w=PITCH)[:, :, 0:HX],
+                in1=half_odd[u % MERGE_SETS][:, PAD - 1 : PAD - 1 + n * PITCH].rearrange(
                     "p (h w) -> p h w", w=PITCH
                 )[:, :, 0:HX],
                 op=ADD,
             )
-            for img in range(2):
-                nc.sync.dma_start(
-                    out=out[2 * pair + img].rearrange("c h w -> c (h w)"), in_=res[img:P:2, :]
-                )
+            for pair, h0, h1, at in segments(n * u, n * (u + 1)):
+                for img in range(2):
+                    nc.sync.dma_start(
+                        out=out[2 * pair + img].rearrange("c h w -> c (h w)")[:, h0 * HX : h1 * HX],
+                        in_=res[img:P:2, at * HX : (at + h1 - h0) * HX],
+                    )
+
+        def start_single(k):
+            nc.sync.dma_start(
+                out=partner[0:P:2, PAD:], in_=sums[1:P:2, k].rearrange("p n f -> p (n f)")
+            )
+
+        def finish_single(k):
+            res = keep.tile([P, 2, WIN_ROWS * HX], F32, name="single")
+            nc.vector.tensor_tensor(
+                out=res[:].rearrange("p n (r w) -> p n r w", w=HX),
+                in0=sums[:, k].rearrange("p n (r w) -> p n r w", w=PITCH)[:, :, :, 0:HX],
+                in1=partner[:, PAD - 1 : PAD - 1 + 2 * SLOT].rearrange("p (n r w) -> p n r w", n=2, w=PITCH)[
+                    :, :, :, 0:HX
+                ],
+                op=ADD,
+            )
+            store_pair(nc.sync, res, WIN_ROWS * k, WIN_ROWS * (k + 1))
 
         for n in range(2):
             load_rows(n, 0, 2 * CHUNK_ROWS)
@@ -295,7 +281,7 @@ def tile_sparseconv2d_t_kernel(tc, x, weight, bias, grad_out, out):
             load_rows(n, 0, HG)
 
         group = PERIOD * ROW_COLS
-        zeros = (FRONT + LEAD) * ROW_COLS
+        zeros = LEAD * ROW_COLS
         body = PAIRS * group
         for plane, per_word in ((g_codes[:].bitcast(I32), 1), (g_scales[:].bitcast(I32), 4)):
             nc.vector.memset(
@@ -304,16 +290,16 @@ def tile_sparseconv2d_t_kernel(tc, x, weight, bias, grad_out, out):
                 ],
                 0,
             )
-            nc.vector.memset(plane[:, body // per_word : (body + zeros) // per_word], 0)
+            nc.vector.memset(plane[:, body // per_word : PLANE_COLS // per_word], 0)
         nc.vector.memset(
             sums[:].rearrange("p k n (r w) -> p (k n r) w", w=PITCH)[:, :, HG:PITCH], 0.0
         )
         nc.vector.memset(x_codes[:, 2 * KS * P - 1 :].bitcast(I32), 0)
         nc.vector.memset(x_scales[:, 2 * KS * P - 4 :].bitcast(I32), 0)
         nc.vector.memset(final[:].rearrange("p n (r w) -> p (n r) w", w=HX)[:, :, HG:HX], 0.0)
-        nc.vector.memset(half_odd[:, 0:PAD], 0.0)
-        for part in last_parts:
-            nc.vector.memset(partner[part][:, 0:PAD], 0.0)
+        for tile in half_odd:
+            nc.vector.memset(tile[:, 0:PAD], 0.0)
+        nc.vector.memset(partner[:], 0.0)
 
         copy_chunk(0, SHARES_START)
         copy_chunk(1, SHARES_START)
@@ -343,14 +329,8 @@ def tile_sparseconv2d_t_kernel(tc, x, weight, bias, grad_out, out):
         weight_quantise(1, 2, 2)
         copy_chunk(2, SHARES)
 
-        started = {}
-
-        def finishes(k, engine):
-            for part in parts:
-                if started.get(part, k) == k - MERGE_LAG:
-                    finish_merge(part, engine)
-
-        for k in range(N_WIN + MERGE_LAG):
+        single = N_WIN - 2
+        for k in range(single):
             if k + COPY_AHEAD < N_CHUNKS:
                 copy_chunk(k + COPY_AHEAD, SHARES)
             if k + QUANT_AHEAD < N_CHUNKS:
@@ -359,22 +339,26 @@ def tile_sparseconv2d_t_kernel(tc, x, weight, bias, grad_out, out):
                 shift_codes()
             if k == SHIFT_AT + 1:
                 shift_scales()
-            if k == N_WIN - 1:
-                last_window()
-                finishes(k, "gpsimd")
-                continue
-            wins = []
-            if k < N_WIN - PAIR_WINS + 1:
-                if k % 2 == 1:
-                    wins = [k - 1, k]
-            elif k < N_WIN:
-                wins = [k]
-            if wins:
-                matmuls(wins)
-            for kk in wins:
-                evacuate(kk)
-            for part in parts:
-                if part[2] - 1 in wins:
-                    start_merge(part)
-                    started[part] = k
-            finishes(k, "gpsimd" if k >= N_WIN else "vector")
+            if k % UNIT == UNIT - 1:
+                matmuls(list(range(k + 1 - UNIT, k + 1)))
+                for kk in range(k + 1 - UNIT, k + 1):
+                    evacuate(kk)
+                start_merge(k // UNIT)
+            if k >= MERGE_LAG and (k - MERGE_LAG) % UNIT == UNIT - 1:
+                finish_merge((k - MERGE_LAG) // UNIT)
+
+        matmuls([single])
+        evacuate(single)
+        start_single(single)
+        finish_merge(single // UNIT - 2)
+        last_group(0)
+        last_sum(0)
+        last_group(1)
+        last_sum(1)
+        finish_merge(single // UNIT - 1)
+        last_group(2)
+        last_sum(2)
+        last_group(3)
+        finish_single(single)
+        last_sum(3)
+        store_pair(nc.scalar, final, WIN_ROWS * (N_WIN - 1), OUT_ROWS)

@@ -64,7 +64,6 @@ def tile_sparseconv2d_t_kernel(tc, x, weight, bias, grad_out, out):
     with ExitStack() as ctx:
         keep = ctx.enter_context(tc.tile_pool(name="keep", bufs=1))
         grouped = ctx.enter_context(tc.tile_pool(name="grouped", bufs=4))
-        results = ctx.enter_context(tc.tile_pool(name="results", bufs=4))
         banks = ctx.enter_context(tc.psum_pool(name="banks", bufs=8))
         ctx.enter_context(tc.manual_schedule())
 
@@ -85,6 +84,7 @@ def tile_sparseconv2d_t_kernel(tc, x, weight, bias, grad_out, out):
             keep.tile([P, PAD + UNIT * SLOT], F32, name="odd%d" % n, align_bytes=64) for n in range(MERGE_SETS)
         ]
         partner = keep.tile([P, PAD + 2 * SLOT], F32, align_bytes=64)
+        results = keep.tile([P, (N_WIN - 2) * WIN_ROWS * HX], F32, align_bytes=64)
 
         raw = {}
         whole = {}
@@ -233,20 +233,22 @@ def tile_sparseconv2d_t_kernel(tc, x, weight, bias, grad_out, out):
 
         def finish_merge(u):
             n = UNIT * WIN_ROWS
-            res = results.tile([P, n * HX], F32, name="res")
             nc.vector.tensor_tensor(
-                out=res[:].rearrange("p (h w) -> p h w", w=HX),
+                out=results[:, n * u * HX : n * (u + 1) * HX].rearrange("p (h w) -> p h w", w=HX),
                 in0=half_even[u % MERGE_SETS][:].rearrange("p (h w) -> p h w", w=PITCH)[:, :, 0:HX],
                 in1=half_odd[u % MERGE_SETS][:, PAD - 1 : PAD - 1 + n * PITCH].rearrange(
                     "p (h w) -> p h w", w=PITCH
                 )[:, :, 0:HX],
                 op=ADD,
             )
-            for pair, h0, h1, at in segments(n * u, n * (u + 1)):
+            for pair in range(PAIRS):
+                r0, r1 = PERIOD * pair, min(PERIOD * (pair + 1), (N_WIN - 2) * WIN_ROWS)
+                if not n * u < r1 <= n * (u + 1):
+                    continue
                 for img in range(2):
                     nc.sync.dma_start(
-                        out=out[2 * pair + img].rearrange("c h w -> c (h w)")[:, h0 * HX : h1 * HX],
-                        in_=res[img:P:2, at * HX : (at + h1 - h0) * HX],
+                        out=out[2 * pair + img].rearrange("c h w -> c (h w)")[:, 0 : (r1 - r0) * HX],
+                        in_=results[img:P:2, r0 * HX : r1 * HX],
                     )
 
         def start_single(k):

@@ -36,15 +36,15 @@ UNIT = 2
 PITCH = 36
 SLOT = WIN_ROWS * PITCH
 PAD = 4
-SHARES_START = (("vector", 0, 0, 8), ("scalar", 1, 0, 4), ("gpsimd", 1, 4, 8))
+SHARES_START = (("vector", 0, 0, 8), ("scalar", 1, 0, 4), ("vector", 1, 4, 8))
+SHARES_NEXT = (("vector", 0, 0, 8), ("scalar", 1, 0, 8))
 SHARES = (("vector", 0, 0, 4), ("gpsimd", 0, 4, 8), ("scalar", 1, 0, 8))
 COPY_AHEAD, QUANT_AHEAD = 3, 2
 MERGE_LAG = 4
-MERGE_SETS = 3
+MERGE_SETS = 4
 WARM_UP = 8
 SHIFT_AT = 3
 F_LEN = C * KS * KS
-SHIFT_AT = 3
 
 FLOPS = 2 * CO * C * KS * KS * N_IMG * HG * HG
 BYTES = CO * C * KS * KS * 2 + N_IMG * CO * HG * HG * 2 + N_IMG * C * HX * HX * 4
@@ -282,6 +282,10 @@ def tile_sparseconv2d_t_kernel(tc, x, weight, bias, grad_out, out):
         for n in range(4, N_IMG):
             load_rows(n, 0, HG)
 
+        early = keep.tile([P, 3, 16], F32)
+        nc.vector.memset(early[:, 0], 0.0)
+        nc.scalar.copy(out=early[:, 1], in_=early[:, 0])
+        nc.gpsimd.tensor_scalar(out=early[:, 2], in0=early[:, 0], scalar1=1.0, scalar2=0.0, op0=MULT, op1=ADD)
         group = PERIOD * ROW_COLS
         zeros = LEAD * ROW_COLS
         body = PAIRS * group
@@ -329,12 +333,12 @@ def tile_sparseconv2d_t_kernel(tc, x, weight, bias, grad_out, out):
         weight_copy("scalar", 1, 3)
         weight_quantise(1, 0, 2)
         weight_quantise(1, 2, 2)
-        copy_chunk(2, SHARES)
+        copy_chunk(2, SHARES_NEXT)
 
         single = N_WIN - 2
         for k in range(single):
             if k + COPY_AHEAD < N_CHUNKS:
-                copy_chunk(k + COPY_AHEAD, SHARES)
+                copy_chunk(k + COPY_AHEAD, SHARES_NEXT if k <= 1 else SHARES)
             if k + QUANT_AHEAD < N_CHUNKS:
                 quantise_chunk(k + QUANT_AHEAD)
             if k == SHIFT_AT:
@@ -346,8 +350,8 @@ def tile_sparseconv2d_t_kernel(tc, x, weight, bias, grad_out, out):
                 for kk in range(k + 1 - UNIT, k + 1):
                     evacuate(kk)
                 start_merge(k // UNIT)
-            if k >= MERGE_LAG and (k - MERGE_LAG) % UNIT == UNIT - 1:
-                finish_merge((k - MERGE_LAG) // UNIT)
+            for u in {8: [0], 9: [1], 10: [2], 11: [3], 13: [4], 15: [5]}.get(k, ()):
+                finish_merge(u)
 
         matmuls([single])
         evacuate(single)

@@ -10,7 +10,6 @@ U8 = mybir.dt.uint8
 E4M3_X4 = mybir.dt.float8_e4m3fn_x4
 E5M2_X4 = mybir.dt.float8_e5m2_x4
 ADD = mybir.AluOpType.add
-MULT = mybir.AluOpType.mult
 
 P = 128
 PACK = 4
@@ -36,14 +35,11 @@ UNIT = 2
 PITCH = 36
 SLOT = WIN_ROWS * PITCH
 PAD = 4
-SHARES_START = (("vector", 0, 0, 8), ("scalar", 1, 0, 4), ("vector", 1, 4, 8))
-SHARES_NEXT = (("vector", 0, 0, 8), ("scalar", 1, 0, 8))
-SHARES = (("vector", 0, 0, 4), ("gpsimd", 0, 4, 8), ("scalar", 1, 0, 8))
-COPY_AHEAD, QUANT_AHEAD = 3, 2
-MERGE_LAG = 4
+SHARES_NEXT = (("vector", 0, 0, 8), ("scalar", 1, 0, 4), ("vector", 1, 4, 8))
+SHARES = (("vector", 0, 0, 8), ("scalar", 1, 0, 8))
 MERGE_SETS = 4
 WARM_UP = 8
-SHIFT_AT = 3
+SHIFT_AT = 13
 F_LEN = C * KS * KS
 
 FLOPS = 2 * CO * C * KS * KS * N_IMG * HG * HG
@@ -72,7 +68,7 @@ def tile_sparseconv2d_t_kernel(tc, x, weight, bias, grad_out, out):
         w_raw = keep.tile([P, PACK * F_LEN], BF16)
         x_codes = keep.tile([P, 2 * KS * P], U32, align_bytes=64)
         x_scales = keep.tile([P, 2 * KS * P], U8, align_bytes=64)
-        final = keep.tile([P, 2, LAST_ROWS * HX], F32, align_bytes=64)
+        final = keep.tile([P, 2, (WIN_ROWS + LAST_ROWS) * HX], F32, align_bytes=64)
         w_grp = keep.tile([P, 2, KS, C, 2, PACK], BF16, align_bytes=64)
         w_codes = keep.tile([P, 2 * KS * P], U32, align_bytes=64)
         w_scales = keep.tile([P, 2 * KS * P], U8, align_bytes=64)
@@ -103,20 +99,11 @@ def tile_sparseconv2d_t_kernel(tc, x, weight, bias, grad_out, out):
 
         def copy_chunk(j, shares):
             pair, part = divmod(j, CHUNKS_PER_PAIR)
-            grp[j] = grouped.tile([P, CHUNK_ROWS, 2, HG, PACK], BF16, name="grp", align_bytes=64)
+            if j not in grp:
+                grp[j] = grouped.tile([P, CHUNK_ROWS, 2, HG, PACK], BF16, name="grp", align_bytes=64)
             for engine, img, r0, r1 in shares:
                 src = raw[2 * pair + img, CHUNK_ROWS * part][:, :, r0 * HG : r1 * HG]
                 dst = grp[j][:, r0:r1, img]
-                if engine == "gpsimd":
-                    nc.gpsimd.tensor_scalar(
-                        out=dst,
-                        in0=src.rearrange("p t (r q) -> p r q t", q=HG),
-                        scalar1=1.0,
-                        scalar2=0.0,
-                        op0=MULT,
-                        op1=ADD,
-                    )
-                    continue
                 dst4 = dst.rearrange("p r (c i) t -> p r c t i", i=4)
                 src4 = src.rearrange("p t (r c i) -> p r c t i", c=HG // 4, i=4)
                 if engine == "vector":
@@ -207,7 +194,8 @@ def tile_sparseconv2d_t_kernel(tc, x, weight, bias, grad_out, out):
 
         def last_sum(s):
             src = acc[N_WIN - 1, s][:, 0 : LAST_ROWS * ROW_COLS].rearrange("p (r n q) -> p r n q", n=2, q=HG)
-            dst = final[:].rearrange("p n (r w) -> p r n w", w=HX)[:, :, :, s : s + HG]
+            rows = final[:].rearrange("p n (r w) -> p r n w", w=HX)[:, WIN_ROWS:]
+            dst = rows[:, :, :, s : s + HG]
             if s == 0:
                 nc.scalar.copy(out=dst, in_=src)
             else:
@@ -257,16 +245,14 @@ def tile_sparseconv2d_t_kernel(tc, x, weight, bias, grad_out, out):
             )
 
         def finish_single(k):
-            res = keep.tile([P, 2, WIN_ROWS * HX], F32, name="single")
             nc.vector.tensor_tensor(
-                out=res[:].rearrange("p n (r w) -> p n r w", w=HX),
+                out=final[:].rearrange("p n (r w) -> p n r w", w=HX)[:, :, 0:WIN_ROWS],
                 in0=sums[:, k].rearrange("p n (r w) -> p n r w", w=PITCH)[:, :, :, 0:HX],
                 in1=partner[:, PAD - 1 : PAD - 1 + 2 * SLOT].rearrange("p (n r w) -> p n r w", n=2, w=PITCH)[
                     :, :, :, 0:HX
                 ],
                 op=ADD,
             )
-            store_pair(nc.sync, res, WIN_ROWS * k, WIN_ROWS * (k + 1))
 
         for n in range(2):
             load_rows(n, 0, 2 * CHUNK_ROWS)
@@ -282,10 +268,9 @@ def tile_sparseconv2d_t_kernel(tc, x, weight, bias, grad_out, out):
         for n in range(4, N_IMG):
             load_rows(n, 0, HG)
 
-        early = keep.tile([P, 3, 16], F32)
+        early = keep.tile([P, 2, 16], F32)
         nc.vector.memset(early[:, 0], 0.0)
         nc.scalar.copy(out=early[:, 1], in_=early[:, 0])
-        nc.gpsimd.tensor_scalar(out=early[:, 2], in0=early[:, 0], scalar1=1.0, scalar2=0.0, op0=MULT, op1=ADD)
         group = PERIOD * ROW_COLS
         zeros = LEAD * ROW_COLS
         body = PAIRS * group
@@ -302,13 +287,17 @@ def tile_sparseconv2d_t_kernel(tc, x, weight, bias, grad_out, out):
         )
         nc.vector.memset(x_codes[:, 2 * KS * P - 1 :].bitcast(I32), 0)
         nc.vector.memset(x_scales[:, 2 * KS * P - 4 :].bitcast(I32), 0)
-        nc.vector.memset(final[:].rearrange("p n (r w) -> p (n r) w", w=HX)[:, :, HG:HX], 0.0)
+        nc.vector.memset(
+            final[:].rearrange("p n (r w) -> p n r w", w=HX)[:, :, WIN_ROWS:, HG:HX], 0.0
+        )
         for tile in half_odd:
             nc.vector.memset(tile[:, 0:PAD], 0.0)
         nc.vector.memset(partner[:], 0.0)
 
-        copy_chunk(0, SHARES_START)
-        copy_chunk(1, SHARES_START)
+        copy_chunk(0, (("vector", 0, 0, 8),))
+        copy_chunk(1, (("vector", 0, 0, 8),))
+        copy_chunk(0, (("scalar", 1, 0, 4), ("vector", 1, 4, 8)))
+        copy_chunk(1, (("scalar", 1, 0, 4), ("vector", 1, 4, 8)))
         warm = banks.tile([P, WIN_COLS], F32, name="acc")
         for w_i in range(WARM_UP):
             nc.tensor.matmul(
@@ -333,38 +322,38 @@ def tile_sparseconv2d_t_kernel(tc, x, weight, bias, grad_out, out):
         weight_copy("scalar", 1, 3)
         weight_quantise(1, 0, 2)
         weight_quantise(1, 2, 2)
-        copy_chunk(2, SHARES_NEXT)
 
         single = N_WIN - 2
         for k in range(single):
-            if k + COPY_AHEAD < N_CHUNKS:
-                copy_chunk(k + COPY_AHEAD, SHARES_NEXT if k <= 1 else SHARES)
-            if k + QUANT_AHEAD < N_CHUNKS:
-                quantise_chunk(k + QUANT_AHEAD)
-            if k == SHIFT_AT:
-                shift_codes()
-            if k == SHIFT_AT + 1:
-                shift_scales()
+            if k % UNIT == 0 and k + UNIT < N_CHUNKS:
+                for j in range(k + UNIT, k + 2 * UNIT):
+                    copy_chunk(j, SHARES_NEXT if j == 3 else SHARES)
+                for j in range(k + UNIT, k + 2 * UNIT):
+                    quantise_chunk(j)
+            if k == single - UNIT:
+                finish_merge(k // UNIT - 1)
             if k % UNIT == UNIT - 1:
                 matmuls(list(range(k + 1 - UNIT, k + 1)))
                 for kk in range(k + 1 - UNIT, k + 1):
                     evacuate(kk)
                 start_merge(k // UNIT)
-            for u in {8: [0], 9: [1], 10: [2], 11: [3], 13: [4], 15: [5]}.get(k, ()):
+            for u in {8: [0], 9: [1], 10: [2], 11: [3], 13: [4, 5]}.get(k, ()):
                 finish_merge(u)
+            if k == SHIFT_AT:
+                shift_codes()
+                shift_scales()
 
         matmuls([single])
         evacuate(single)
         start_single(single)
-        finish_merge(single // UNIT - 2)
+        finish_merge(single // UNIT - 1)
         last_group(0)
         last_sum(0)
         last_group(1)
         last_sum(1)
-        finish_merge(single // UNIT - 1)
+        finish_single(single)
         last_group(2)
         last_sum(2)
         last_group(3)
-        finish_single(single)
         last_sum(3)
-        store_pair(nc.scalar, final, WIN_ROWS * (N_WIN - 1), OUT_ROWS)
+        store_pair(nc.scalar, final, WIN_ROWS * single, OUT_ROWS)

@@ -35,10 +35,12 @@ UNIT = 2
 PITCH = 36
 SLOT = WIN_ROWS * PITCH
 PAD = 4
+SHARES_ODD = (("vector", 0, 0, 6), ("scalar", 0, 6, 8), ("scalar", 1, 0, 8))
 SHARES_NEXT = (("vector", 0, 0, 8), ("scalar", 1, 0, 4), ("vector", 1, 4, 8))
 SHARES = (("vector", 0, 0, 8), ("scalar", 1, 0, 8))
 MERGE_SETS = 4
 WARM_UP = 8
+STORED_AT = {11: 0, 13: 1, 15: 2}
 SHIFT_AT = 13
 F_LEN = C * KS * KS
 
@@ -229,15 +231,14 @@ def tile_sparseconv2d_t_kernel(tc, x, weight, bias, grad_out, out):
                 )[:, :, 0:HX],
                 op=ADD,
             )
-            for pair in range(PAIRS):
-                r0, r1 = PERIOD * pair, min(PERIOD * (pair + 1), (N_WIN - 2) * WIN_ROWS)
-                if not n * u < r1 <= n * (u + 1):
-                    continue
-                for img in range(2):
-                    nc.sync.dma_start(
-                        out=out[2 * pair + img].rearrange("c h w -> c (h w)")[:, 0 : (r1 - r0) * HX],
-                        in_=results[img:P:2, r0 * HX : r1 * HX],
-                    )
+
+        def store_rows(engine, pair):
+            r0, r1 = PERIOD * pair, min(PERIOD * (pair + 1), (N_WIN - 2) * WIN_ROWS)
+            for img in range(2):
+                engine.dma_start(
+                    out=out[2 * pair + img].rearrange("c h w -> c (h w)")[:, 0 : (r1 - r0) * HX],
+                    in_=results[img:P:2, r0 * HX : r1 * HX],
+                )
 
         def start_single(k):
             nc.sync.dma_start(
@@ -327,18 +328,18 @@ def tile_sparseconv2d_t_kernel(tc, x, weight, bias, grad_out, out):
         for k in range(single):
             if k % UNIT == 0 and k + UNIT < N_CHUNKS:
                 for j in range(k + UNIT, k + 2 * UNIT):
-                    copy_chunk(j, SHARES_NEXT if j == 3 else SHARES)
+                    copy_chunk(j, SHARES_NEXT if j == 3 else SHARES_ODD if j > 3 and j % 2 else SHARES)
                 for j in range(k + UNIT, k + 2 * UNIT):
                     quantise_chunk(j)
-            if k == single - UNIT:
-                finish_merge(k // UNIT - 1)
             if k % UNIT == UNIT - 1:
                 matmuls(list(range(k + 1 - UNIT, k + 1)))
                 for kk in range(k + 1 - UNIT, k + 1):
                     evacuate(kk)
                 start_merge(k // UNIT)
-            for u in {8: [0], 9: [1], 10: [2], 11: [3], 13: [4, 5]}.get(k, ()):
+            for u in {8: [0], 9: [1], 10: [2], 11: [3], 13: [4, 5], 15: [6]}.get(k, ()):
                 finish_merge(u)
+            if k in STORED_AT:
+                store_rows(nc.scalar, STORED_AT[k])
             if k == SHIFT_AT:
                 shift_codes()
                 shift_scales()
@@ -346,11 +347,12 @@ def tile_sparseconv2d_t_kernel(tc, x, weight, bias, grad_out, out):
         matmuls([single])
         evacuate(single)
         start_single(single)
-        finish_merge(single // UNIT - 1)
         last_group(0)
         last_sum(0)
         last_group(1)
         last_sum(1)
+        finish_merge(single // UNIT - 1)
+        store_rows(nc.sync, PAIRS - 1)
         finish_single(single)
         last_group(2)
         last_sum(2)

from contextlib import ExitStack

import concourse.mybir as mybir

BF16 = mybir.dt.bfloat16
F32 = mybir.dt.float32
I32 = mybir.dt.int32
U32 = mybir.dt.uint32
U8 = mybir.dt.uint8
E4M3_X4 = mybir.dt.float8_e4m3fn_x4
E5M2_X4 = mybir.dt.float8_e5m2_x4
ADD = mybir.AluOpType.add

P = 128
PACK = 4
N_IMG, C, CO = 8, 64, 512
KS = 4
HG = 32
HX = HG + KS - 1
PAIRS = N_IMG // 2
ROW_COLS = 2 * HG
LEAD = KS - 1
PERIOD = HG + LEAD
WIN_ROWS = 8
WIN_COLS = WIN_ROWS * ROW_COLS
OUT_ROWS = PAIRS * PERIOD
N_WIN = -(-OUT_ROWS // WIN_ROWS)
LAST_ROWS = OUT_ROWS - (N_WIN - 1) * WIN_ROWS
PLANE_ROWS = LEAD + N_WIN * WIN_ROWS
PLANE_COLS = PLANE_ROWS * ROW_COLS
CHUNK_ROWS = 8
CHUNKS_PER_PAIR = HG // CHUNK_ROWS
N_CHUNKS = PAIRS * CHUNKS_PER_PAIR
UNIT = 2
PITCH = 36
SLOT = WIN_ROWS * PITCH
PAD = 4
SHARES_ODD = (("vector", 0, 0, 6), ("scalar", 0, 6, 8), ("scalar", 1, 0, 8))
SHARES_NEXT = (("vector", 0, 0, 8), ("scalar", 1, 0, 4), ("vector", 1, 4, 8))
SHARES = (("vector", 0, 0, 8), ("scalar", 1, 0, 8))
MERGE_SETS = 4
WARM_UP = 8
STORED_AT = {11: 0, 13: 1, 15: 2}
SHIFT_AT = 13
F_LEN = C * KS * KS

FLOPS = 2 * CO * C * KS * KS * N_IMG * HG * HG
BYTES = CO * C * KS * KS * 2 + N_IMG * CO * HG * HG * 2 + N_IMG * C * HX * HX * 4


def segments(r0, r1):
    found = []
    for pair in range(PAIRS):
        a, b = max(r0, PERIOD * pair), min(r1, PERIOD * (pair + 1))
        if a < b:
            found.append((pair, a - PERIOD * pair, b - PERIOD * pair, a - r0))
    return found


def tile_sparseconv2d_t_kernel(tc, x, weight, bias, grad_out, out):
    nc = tc.nc
    with ExitStack() as ctx:
        keep = ctx.enter_context(tc.tile_pool(name="keep", bufs=1))
        grouped = ctx.enter_context(tc.tile_pool(name="grouped", bufs=4))
        banks = ctx.enter_context(tc.psum_pool(name="banks", bufs=8))
        ctx.enter_context(tc.manual_schedule())

        g_codes = keep.tile([P, PLANE_COLS], U32, align_bytes=64)
        g_scales = keep.tile([P, PLANE_COLS], U8, align_bytes=64)
        w_raw = keep.tile([P, PACK * F_LEN], BF16)
        x_codes = keep.tile([P, 2 * KS * P], U32, align_bytes=64)
        x_scales = keep.tile([P, 2 * KS * P], U8, align_bytes=64)
        final = keep.tile([P, 2, (WIN_ROWS + LAST_ROWS) * HX], F32, align_bytes=64)
        w_grp = keep.tile([P, 2, KS, C, 2, PACK], BF16, align_bytes=64)
        w_codes = keep.tile([P, 2 * KS * P], U32, align_bytes=64)
        w_scales = keep.tile([P, 2 * KS * P], U8, align_bytes=64)
        sums = keep.tile([P, N_WIN - 1, 2, SLOT], F32, align_bytes=64)
        half_even = [
            keep.tile([P, UNIT * SLOT], F32, name="even%d" % n, align_bytes=64) for n in range(MERGE_SETS)
        ]
        half_odd = [
            keep.tile([P, PAD + UNIT * SLOT], F32, name="odd%d" % n, align_bytes=64) for n in range(MERGE_SETS)
        ]
        partner = keep.tile([P, PAD + 2 * SLOT], F32, align_bytes=64)
        results = keep.tile([P, (N_WIN - 2) * WIN_ROWS * HX], F32, align_bytes=64)

        raw = {}
        whole = {}
        grp = {}
        acc = {}

        def load_rows(n, r0, r1):
            tile = keep.tile([P, PACK, (r1 - r0) * HG], BF16, name="raw%d_%d" % (n, r0))
            nc.sync.dma_start(
                out=tile[:],
                in_=grad_out[n, :, r0:r1, :].rearrange("(p t) h w -> p t (h w)", t=PACK),
            )
            whole[n, r0] = tile
            for r in range(r0, r1, CHUNK_ROWS):
                raw[n, r] = tile[:, :, (r - r0) * HG : (r - r0 + CHUNK_ROWS) * HG]

        def copy_chunk(j, shares):
            pair, part = divmod(j, CHUNKS_PER_PAIR)
            if j not in grp:
                grp[j] = grouped.tile([P, CHUNK_ROWS, 2, HG, PACK], BF16, name="grp", align_bytes=64)
            for engine, img, r0, r1 in shares:
                src = raw[2 * pair + img, CHUNK_ROWS * part][:, :, r0 * HG : r1 * HG]
                dst = grp[j][:, r0:r1, img]
                dst4 = dst.rearrange("p r (c i) t -> p r c t i", i=4)
                src4 = src.rearrange("p t (r c i) -> p r c t i", c=HG // 4, i=4)
                if engine == "vector":
                    nc.vector.tensor_copy(out=dst4, in_=src4)
                else:
                    nc.scalar.copy(out=dst4, in_=src4)

        def quantise_chunk(j):
            pair, part = divmod(j, CHUNKS_PER_PAIR)
            c0 = (LEAD + PERIOD * pair + CHUNK_ROWS * part) * ROW_COLS
            cols = slice(c0, c0 + CHUNK_ROWS * ROW_COLS)
            nc.vector.quantize_mx(
                out=g_codes[:, cols].bitcast(E5M2_X4),
                scales=g_scales[:, cols],
                in_=grp[j][:].rearrange("p r n q t -> p (r n q t)"),
            )

        def weight_copy(engine, a, i):
            w_src = w_raw[:].rearrange(
                "p (t c i a b) -> p t c i a b", t=PACK, i=KS, a=2, b=2
            )
            view = w_src[:, :, :, i, a, :].rearrange("p t c b -> p c b t")
            if engine == "vector":
                nc.vector.tensor_copy(out=w_grp[:, a, i], in_=view)
            else:
                nc.scalar.copy(out=w_grp[:, a, i], in_=view)

        def shift_codes():
            n = 2 * KS * P - 1
            nc.vector.tensor_copy(out=x_codes[:, 0:n].bitcast(I32), in_=w_codes[:, 1 : n + 1].bitcast(I32))

        def shift_scales():
            n = 2 * KS * P - 1
            nc.vector.tensor_copy(out=x_scales[:, 0:n], in_=w_scales[:, 1 : n + 1])

        def weight_quantise(a, i0, n):
            c0 = (a * KS + i0) * P
            nc.vector.quantize_mx(
                out=w_codes[:, c0 : c0 + n * P].bitcast(E4M3_X4),
                scales=w_scales[:, c0 : c0 + n * P],
                in_=w_grp[:, a, i0 : i0 + n].rearrange("p i c b t -> p (i c b t)"),
            )

        def matmuls(wins):
            for a in range(2):
                for k in wins:
                    acc[k, a] = banks.tile([P, WIN_COLS], F32, name="acc")
                for i in range(KS):
                    s0 = (a * KS + i) * P
                    for k in wins:
                        c0 = WIN_COLS * k + ROW_COLS * (LEAD - i)
                        nc.tensor.matmul_mx(
                            out=acc[k, a][:],
                            lhsT=w_codes[:, s0 : s0 + P].bitcast(E4M3_X4),
                            lhsT_scale=w_scales[:, s0 : s0 + P],
                            rhs=g_codes[:, c0 : c0 + WIN_COLS].bitcast(E5M2_X4),
                            rhs_scale=g_scales[:, c0 : c0 + WIN_COLS],
                            start=(i == 0),
                            stop=(i == KS - 1),
                        )

        def evacuate(k):
            slot = sums[:, k].rearrange("p n (r w) -> p r n w", w=PITCH)
            for a in range(2):
                src = acc[k, a][:].rearrange("p (r n q) -> p r n q", n=2, q=HG)
                dst = slot[:, :, :, 2 * a : 2 * a + HG]
                if a == 0:
                    nc.scalar.copy(out=dst, in_=src)
                else:
                    nc.vector.tensor_tensor(out=dst, in0=src, in1=dst, op=ADD)

        def last_group(s):
            k = N_WIN - 1
            acc[k, s] = banks.tile([P, WIN_COLS], F32, name="acc")
            codes, scales = (w_codes, w_scales) if s % 2 == 0 else (x_codes, x_scales)
            for i in range(KS):
                c0 = WIN_COLS * k + ROW_COLS * (LEAD - i)
                s0 = ((s // 2) * KS + i) * P
                nc.tensor.matmul_mx(
                    out=acc[k, s][:],
                    lhsT=codes[:, s0 : s0 + P].bitcast(E4M3_X4),
                    lhsT_scale=scales[:, s0 : s0 + P],
                    rhs=g_codes[:, c0 : c0 + WIN_COLS].bitcast(E5M2_X4),
                    rhs_scale=g_scales[:, c0 : c0 + WIN_COLS],
                    start=(i == 0),
                    stop=(i == KS - 1),
                )

        def last_sum(s):
            src = acc[N_WIN - 1, s][:, 0 : LAST_ROWS * ROW_COLS].rearrange("p (r n q) -> p r n q", n=2, q=HG)
            rows = final[:].rearrange("p n (r w) -> p r n w", w=HX)[:, WIN_ROWS:]
            dst = rows[:, :, :, s : s + HG]
            if s == 0:
                nc.scalar.copy(out=dst, in_=src)
            else:
                nc.vector.tensor_tensor(out=dst, in0=src, in1=dst, op=ADD)

        def store_pair(engine, tile, r0, r1):
            for pair, h0, h1, at in segments(r0, r1):
                engine.dma_start(
                    out=out[2 * pair : 2 * pair + 2].rearrange("n c h w -> c n (h w)")[:, :, h0 * HX : h1 * HX],
                    in_=tile[0:P:2, :, at * HX : (at + h1 - h0) * HX],
                )

        def start_merge(u):
            for img in range(2):
                nc.sync.dma_start(
                    out=half_even[u % MERGE_SETS][img:P:2, :].rearrange("p (k f) -> p k f", f=SLOT),
                    in_=sums[0:P:2, UNIT * u : UNIT * (u + 1), img, :],
                )
                nc.sync.dma_start(
                    out=half_odd[u % MERGE_SETS][img:P:2, PAD:].rearrange("p (k f) -> p k f", f=SLOT),
                    in_=sums[1:P:2, UNIT * u : UNIT * (u + 1), img, :],
                )

        def finish_merge(u):
            n = UNIT * WIN_ROWS
            nc.vector.tensor_tensor(
                out=results[:, n * u * HX : n * (u + 1) * HX].rearrange("p (h w) -> p h w", w=HX),
                in0=half_even[u % MERGE_SETS][:].rearrange("p (h w) -> p h w", w=PITCH)[:, :, 0:HX],
                in1=half_odd[u % MERGE_SETS][:, PAD - 1 : PAD - 1 + n * PITCH].rearrange(
                    "p (h w) -> p h w", w=PITCH
                )[:, :, 0:HX],
                op=ADD,
            )

        def store_rows(engine, pair):
            r0, r1 = PERIOD * pair, min(PERIOD * (pair + 1), (N_WIN - 2) * WIN_ROWS)
            for img in range(2):
                engine.dma_start(
                    out=out[2 * pair + img].rearrange("c h w -> c (h w)")[:, 0 : (r1 - r0) * HX],
                    in_=results[img:P:2, r0 * HX : r1 * HX],
                )

        def start_single(k):
            nc.sync.dma_start(
                out=partner[0:P:2, PAD:], in_=sums[1:P:2, k].rearrange("p n f -> p (n f)")
            )

        def finish_single(k):
            nc.vector.tensor_tensor(
                out=final[:].rearrange("p n (r w) -> p n r w", w=HX)[:, :, 0:WIN_ROWS],
                in0=sums[:, k].rearrange("p n (r w) -> p n r w", w=PITCH)[:, :, :, 0:HX],
                in1=partner[:, PAD - 1 : PAD - 1 + 2 * SLOT].rearrange("p (n r w) -> p n r w", n=2, w=PITCH)[
                    :, :, :, 0:HX
                ],
                op=ADD,
            )

        for n in range(2):
            load_rows(n, 0, 2 * CHUNK_ROWS)
        nc.sync.dma_start(
            out=w_raw[:].rearrange("p (t f) -> p t f", t=PACK),
            in_=weight.rearrange("(p t) f -> p t f", t=PACK),
        )
        for n in range(2):
            load_rows(n, 2 * CHUNK_ROWS, HG)
        for r0 in (0, HG // 2):
            for n in range(2, 4):
                load_rows(n, r0, r0 + HG // 2)
        for n in range(4, N_IMG):
            load_rows(n, 0, HG)

        early = keep.tile([P, 2, 16], F32)
        nc.vector.memset(early[:, 0], 0.0)
        nc.scalar.copy(out=early[:, 1], in_=early[:, 0])
        group = PERIOD * ROW_COLS
        zeros = LEAD * ROW_COLS
        body = PAIRS * group
        for plane, per_word in ((g_codes[:].bitcast(I32), 1), (g_scales[:].bitcast(I32), 4)):
            nc.vector.memset(
                plane[:, 0 : body // per_word].rearrange("p (g x) -> p g x", x=group // per_word)[
                    :, :, 0 : zeros // per_word
                ],
                0,
            )
            nc.vector.memset(plane[:, body // per_word : PLANE_COLS // per_word], 0)
        nc.vector.memset(
            sums[:].rearrange("p k n (r w) -> p (k n r) w", w=PITCH)[:, :, HG:PITCH], 0.0
        )
        nc.vector.memset(x_codes[:, 2 * KS * P - 1 :].bitcast(I32), 0)
        nc.vector.memset(x_scales[:, 2 * KS * P - 4 :].bitcast(I32), 0)
        nc.vector.memset(
            final[:].rearrange("p n (r w) -> p n r w", w=HX)[:, :, WIN_ROWS:, HG:HX], 0.0
        )
        for tile in half_odd:
            nc.vector.memset(tile[:, 0:PAD], 0.0)
        nc.vector.memset(partner[:], 0.0)

        copy_chunk(0, (("vector", 0, 0, 8),))
        copy_chunk(1, (("vector", 0, 0, 8),))
        copy_chunk(0, (("scalar", 1, 0, 4), ("vector", 1, 4, 8)))
        copy_chunk(1, (("scalar", 1, 0, 4), ("vector", 1, 4, 8)))
        warm = banks.tile([P, WIN_COLS], F32, name="acc")
        for w_i in range(WARM_UP):
            nc.tensor.matmul(
                out=warm[:],
                lhsT=whole[0, 0][:, 0, 0:P],
                rhs=whole[0, 0][:, 1, 0:WIN_COLS],
                start=True,
                stop=True,
            )
        quantise_chunk(0)
        quantise_chunk(1)
        weight_copy("vector", 0, 0)
        weight_copy("scalar", 0, 1)
        weight_copy("vector", 0, 2)
        weight_copy("scalar", 0, 3)
        weight_quantise(0, 0, 1)
        weight_quantise(0, 1, 1)
        weight_copy("vector", 1, 0)
        weight_copy("scalar", 1, 1)
        weight_quantise(0, 2, 2)
        weight_copy("vector", 1, 2)
        weight_copy("scalar", 1, 3)
        weight_quantise(1, 0, 2)
        weight_quantise(1, 2, 2)

        single = N_WIN - 2
        for k in range(single):
            if k % UNIT == 0 and k + UNIT < N_CHUNKS:
                for j in range(k + UNIT, k + 2 * UNIT):
                    copy_chunk(j, SHARES_NEXT if j == 3 else SHARES_ODD if j > 3 and j % 2 else SHARES)
                for j in range(k + UNIT, k + 2 * UNIT):
                    quantise_chunk(j)
            if k % UNIT == UNIT - 1:
                matmuls(list(range(k + 1 - UNIT, k + 1)))
                for kk in range(k + 1 - UNIT, k + 1):
                    evacuate(kk)
                start_merge(k // UNIT)
            for u in {8: [0], 9: [1], 10: [2], 11: [3], 13: [4, 5], 15: [6]}.get(k, ()):
                finish_merge(u)
            if k in STORED_AT:
                store_rows(nc.scalar, STORED_AT[k])
            if k == SHIFT_AT:
                shift_codes()
                shift_scales()

        matmuls([single])
        evacuate(single)
        start_single(single)
        last_group(0)
        last_sum(0)
        last_group(1)
        last_sum(1)
        finish_merge(single // UNIT - 1)
        store_rows(nc.sync, PAIRS - 1)
        finish_single(single)
        last_group(2)
        last_sum(2)
        last_group(3)
        last_sum(3)
        store_pair(nc.scalar, final, WIN_ROWS * single, OUT_ROWS)
